import numpy as np
import ml_dtypes


def mxq(x, axis, fmt="e4m3"):
    dtype, down = {"e4m3": (ml_dtypes.float8_e4m3fn, 7), "e5m2": (ml_dtypes.float8_e5m2, 14)}[fmt]
    v = np.moveaxis(np.asarray(x, np.float32).astype(ml_dtypes.bfloat16).astype(np.float64), axis, -1)
    blocks = v.reshape(v.shape[:-1] + (-1, 32))
    amax = np.abs(blocks).max(-1, keepdims=True)
    byte = np.maximum(np.where(amax > 0, np.frexp(amax)[1] - 1 + 127, 0) - down, 1)
    scale = np.exp2(byte - 127.0)
    codes = (blocks / scale).astype(np.float32).astype(dtype).astype(np.float64)
    return np.moveaxis((codes * scale).reshape(v.shape), -1, axis)


WIDE = False


def mx_kscale(k):
    if not WIDE:
        return np.ones(k)
    levels = np.array([10, -10, 5, -5, 0])
    a = np.random.permutation(np.resize(levels, k // 512 * 4)).reshape(k // 512, 4)
    idx = np.arange(k)
    return np.exp2(a[idx // 512, idx % 128 // 32])


BF16 = ml_dtypes.bfloat16


def bf(x):
    return np.asarray(x, np.float32).astype(BF16)


def f64(x):
    return np.asarray(x).astype(np.float64)


E2M1 = np.array([0.0, 0.5, 1.0, 1.5, 2.0, 3.0, 4.0, 6.0, -0.0, -0.5, -1.0, -1.5, -2.0, -3.0, -4.0, -6.0])


def pack_weight(w, fmt):
    k, n = w.shape
    w = f64(bf(w)).reshape(k // 32, 32, n)
    amax = np.abs(w).max(1)
    if fmt == "e4m3":
        byte = np.frexp(amax)[1] - 1 + 127 - 7
    else:
        mant, ex = np.frexp(amax / 6.0)
        byte = np.where(mant > 0.5, ex, ex - 1) + 127
    byte = np.clip(np.where(amax > 0, byte, 1), 1, 254)
    scaled = (w * np.exp2(127.0 - byte)[:, None, :]).reshape(k, n).astype(np.float32)
    by_word = np.ascontiguousarray(scaled.reshape(k // 512, 128, 4, n).transpose(0, 1, 3, 2))
    if fmt == "e4m3":
        words = by_word.astype(ml_dtypes.float8_e4m3fn).view(np.uint8)
    else:
        c = by_word.astype(ml_dtypes.float4_e2m1fn).view(np.uint8) & 0xF
        words = c[..., 0::2] | (c[..., 1::2] << 4)
    return np.ascontiguousarray(words), np.ascontiguousarray(byte.astype(np.uint8).reshape(k // 512, 16, n))


def unpack_weight(words, scales, fmt):
    g, p, n, _ = words.shape
    if fmt == "e4m3":
        vals = np.ascontiguousarray(words).view(ml_dtypes.float8_e4m3fn).astype(np.float64)
    else:
        nib = np.empty((g, p, n, 4), np.uint8)
        nib[..., 0::2] = words & 0xF
        nib[..., 1::2] = words >> 4
        vals = E2M1[nib]
    vals = vals * np.repeat(np.exp2(scales.astype(np.float64) - 127.0), 8, axis=1)[..., None]
    return vals.transpose(0, 1, 3, 2).reshape(g * 512, n)


N, D, M, P = 4096, 8, 1024, 1024


def setup_inputs():
    a = np.log2(mx_kscale(M))
    a = a.max() - a
    x = np.random.standard_normal((N, D))
    z = np.random.uniform(0.0, 1.0, (M, D))
    z[:, 0] += a * np.log(2.0)
    g = np.random.standard_normal((M, P)) * 3.2 / np.sqrt(M)
    c = np.triu(g) + 0.25 * np.tril(g, -1) + np.eye(M, P)
    words, scales = pack_weight(c * np.exp2(a)[:, None], "e4m3")
    return {"x": bf(x), "design_points": bf(z), "chol_inv_words": words, "chol_inv_scales": scales}


def reference(x, design_points, chol_inv_words, chol_inv_scales):
    x = f64(x)
    z = f64(design_points)
    mn = np.min(x, axis=0, keepdims=True)
    mx = np.max(x, axis=0, keepdims=True)
    xs = (x - mn) / (mx - mn)
    l1 = np.zeros((x.shape[0], z.shape[0]))
    for d in range(D):
        l1 = l1 + np.abs(xs[:, d][:, None] - z[:, d][None, :])
    k_star = np.exp(-l1)
    return mxq(k_star, 1, "e4m3") @ unpack_weight(chol_inv_words, chol_inv_scales, "e4m3")

@@ -1,0 +1,217 @@
+from contextlib import ExitStack
+
+import concourse.mybir as mybir
+from concourse.masks import make_identity
+
+F32 = mybir.dt.float32
+BF16 = mybir.dt.bfloat16
+I32 = mybir.dt.int32
+U32 = mybir.dt.uint32
+U8 = mybir.dt.uint8
+FP8X4 = mybir.dt.float8_e4m3fn_x4
+ALU = mybir.AluOpType
+ACT = mybir.ActivationFunctionType
+AXIS_X = mybir.AxisListType.X
+
+P = 128
+PACK = 4
+K_PASS = P * PACK
+N_ROWS = 4096
+DIMS = 8
+M_PTS = 1024
+N_COLS = 1024
+PASSES = M_PTS // K_PASS
+SLABS = PASSES * PACK
+N_TILES = N_ROWS // P
+BANK = 512
+HALVES = N_COLS // BANK
+VECTOR_DIMS = 6
+PAIRS = VECTOR_DIMS // 2
+FIXED = DIMS
+
+FLOPS = 2 * N_ROWS * M_PTS * N_COLS
+
+
+def tile_tmgp_sg_kernel(tc, x, design_points, chol_inv_words, chol_inv_scales, out):
+    nc = tc.nc
+    with ExitStack() as stack:
+        const = stack.enter_context(tc.tile_pool(name="const", bufs=1))
+        work = stack.enter_context(tc.tile_pool(name="work", bufs=3))
+        psum_sum = stack.enter_context(tc.psum_pool(name="psum_sum", bufs=4))
+        psum_out = stack.enter_context(tc.psum_pool(name="psum_out", bufs=4))
+
+        identity = const.tile([P, P], F32, name="identity")
+        make_identity(nc, identity[:])
+
+        x_bf = const.tile([P, N_TILES, DIMS], BF16, name="x_bf")
+        nc.sync.dma_start(out=x_bf[:], in_=x.rearrange("(p i) d -> p i d", i=N_TILES))
+        z_bf = const.tile([P, SLABS, DIMS], BF16, name="z_bf")
+        nc.sync.dma_start(
+            out=z_bf[:].rearrange("p (g t) d -> p g (t d)", g=PASSES),
+            in_=design_points.rearrange("(g p t) d -> p g (t d)", g=PASSES, t=PACK),
+        )
+        w_scales = const.tile([P, PASSES, N_COLS], U8, name="w_scales", align_bytes=64)
+        nc.vector.memset(w_scales[:].rearrange("p g n -> p (g n)").bitcast(I32), 0)
+        for g in range(PASSES):
+            for quad in range(4):
+                nc.sync.dma_start(
+                    out=w_scales[32 * quad : 32 * quad + 4, g, :].bitcast(I32),
+                    in_=chol_inv_scales[g, 4 * quad : 4 * quad + 4, :].bitcast(I32),
+                )
+        w_words = const.tile([P, PASSES, N_COLS], U32, name="w_words", align_bytes=64)
+        for g in range(PASSES):
+            nc.sync.dma_start(
+                out=w_words[:, g, :].bitcast(I32),
+                in_=chol_inv_words[g].rearrange("p n t -> p (n t)").bitcast(I32),
+            )
+
+        x32 = const.tile([P, N_TILES, DIMS], F32, name="x32")
+        nc.vector.tensor_copy(out=x32[:], in_=x_bf[:])
+        own = const.tile([P, P], F32, name="own")
+        nc.vector.memset(own[:], 0.0)
+        by_dim = x32[:].rearrange("p i d -> p d i")
+        nc.vector.tensor_reduce(out=own[:, 0:DIMS], in_=by_dim, axis=AXIS_X, op=ALU.max)
+        lowest = const.tile([P, DIMS], F32, name="lowest")
+        nc.vector.tensor_reduce(out=lowest[:], in_=by_dim, axis=AXIS_X, op=ALU.min)
+        nc.vector.tensor_scalar_mul(out=own[:, DIMS : 2 * DIMS], in0=lowest[:], scalar1=-1.0)
+        own_t = psum_sum.tile([P, P], F32, name="own_t", tag="bank")
+        nc.tensor.transpose(out=own_t[:], in_=own[:], identity=identity[:])
+        overall = const.tile([P, 1], F32, name="overall")
+        nc.vector.tensor_reduce(out=overall[:], in_=own_t[:], axis=AXIS_X, op=ALU.max)
+        overall_t = psum_sum.tile([P, P], F32, name="overall_t", tag="bank")
+        nc.tensor.transpose(
+            out=overall_t[:], in_=overall[:, 0:1].to_broadcast([P, P]), identity=identity[:]
+        )
+        bounds = const.tile([P, 2 * DIMS], F32, name="bounds")
+        nc.vector.tensor_copy(out=bounds[:], in_=overall_t[:, 0 : 2 * DIMS])
+        inv_span = const.tile([P, DIMS], F32, name="inv_span")
+        nc.vector.tensor_add(out=inv_span[:], in0=bounds[:, 0:DIMS], in1=bounds[:, DIMS : 2 * DIMS])
+        nc.vector.reciprocal(out=inv_span[:], in_=inv_span[:])
+
+        every_tile = [P, N_TILES, DIMS]
+        xs = const.tile(every_tile, F32, name="xs")
+        nc.vector.tensor_add(
+            out=xs[:], in0=x32[:], in1=bounds[:, DIMS : 2 * DIMS].unsqueeze(1).to_broadcast(every_tile)
+        )
+        nc.vector.tensor_mul(
+            out=xs[:], in0=xs[:], in1=inv_span[:].unsqueeze(1).to_broadcast(every_tile)
+        )
+        neg_half = const.tile(every_tile, F32, name="neg_half")
+        nc.vector.tensor_scalar_mul(out=neg_half[:], in0=xs[:], scalar1=-0.5)
+        pair_shift = const.tile([P, N_TILES, DIMS // 2], F32, name="pair_shift")
+        nc.vector.tensor_reduce(
+            out=pair_shift[:],
+            in_=neg_half[:].rearrange("p i (c e) -> p i c e", e=2),
+            axis=AXIS_X,
+            op=ALU.add,
+        )
+
+        z32 = const.tile([P, SLABS, DIMS + 1], F32, name="z32")
+        nc.vector.tensor_copy(out=z32[:, :, 0:DIMS], in_=z_bf[:])
+        z_sum = const.tile([P, SLABS], F32, name="z_sum")
+        nc.vector.tensor_reduce(out=z_sum[:], in_=z32[:, :, 0:VECTOR_DIMS], axis=AXIS_X, op=ALU.add)
+        nc.vector.tensor_scalar_mul(out=z32[:, :, FIXED], in0=z_sum[:], scalar1=-0.5)
+        rows = const.tile([P, DIMS + 1, M_PTS], F32, name="rows")
+        for r in range(DIMS + 1):
+            for g in range(PASSES):
+                spread = psum_sum.tile([P, PACK, P], F32, name="spread", tag="bank")
+                for t in range(PACK):
+                    nc.tensor.transpose(
+                        out=spread[:, t, :],
+                        in_=z32[:, g * PACK + t, r : r + 1].to_broadcast([P, P]),
+                        identity=identity[:],
+                    )
+                half_row = rows[:, r, g * K_PASS : (g + 1) * K_PASS]
+                if g == 0:
+                    nc.vector.tensor_copy(out=half_row, in_=spread[:].rearrange("p t q -> p (t q)"))
+                else:
+                    nc.scalar.copy(out=half_row, in_=spread[:].rearrange("p t q -> p (t q)"))
+
+        out_tiles = out.rearrange("(p i) c -> i p c", i=N_TILES)
+
+        for i in range(N_TILES):
+            pairs = []
+            for c in range(PAIRS):
+                pair = work.tile([P, M_PTS], F32, name="pair%d" % c)
+                nc.vector.tensor_scalar(
+                    out=pair[:],
+                    in0=rows[:, 2 * c, :],
+                    scalar1=xs[:, i, 2 * c : 2 * c + 1],
+                    scalar2=pair_shift[:, i, c : c + 1],
+                    op0=ALU.max,
+                    op1=ALU.add,
+                )
+                pairs.append(pair)
+            for c in range(PAIRS):
+                nc.vector.scalar_tensor_tensor(
+                    out=pairs[c][:],
+                    in0=rows[:, 2 * c + 1, :],
+                    scalar=xs[:, i, 2 * c + 1 : 2 * c + 2],
+                    in1=pairs[c][:],
+                    op0=ALU.max,
+                    op1=ALU.add,
+                )
+            singles = []
+            for d in range(VECTOR_DIMS, DIMS):
+                single = work.tile([P, M_PTS], F32, name="single%d" % d)
+                nc.scalar.activation(
+                    out=single[:],
+                    in_=rows[:, d, :],
+                    func=ACT.Abs,
+                    scale=0.5,
+                    bias=neg_half[:, i, d : d + 1],
+                )
+                singles.append(single)
+
+            terms = [rows[:, FIXED, :]] + [s[:] for s in singles] + [q[:] for q in pairs]
+            half_l1 = [
+                psum_sum.tile([P, PACK, P], F32, name="half_l1_%d" % g, tag="bank")
+                for g in range(PASSES)
+            ]
+            for k, term in enumerate(terms):
+                for g in range(PASSES):
+                    for t in range(PACK):
+                        slab = g * PACK + t
+                        nc.tensor.matmul(
+                            out=half_l1[g][:, t, :],
+                            lhsT=term[:, slab * P : (slab + 1) * P],
+                            rhs=identity[:],
+                            is_transpose=True,
+                            start=(k == 0 and t == 0),
+                            stop=(k == len(terms) - 1 and t == PACK - 1),
+                        )
+
+            k_star = work.tile([P, PASSES, P, PACK], BF16, name="k_star", align_bytes=64)
+            for g in range(PASSES):
+                nc.scalar.activation(
+                    out=k_star[:, g, :, :],
+                    in_=half_l1[g][:].rearrange("p t n -> p n t"),
+                    func=ACT.Exp,
+                    scale=-2.0,
+                )
+            k_words = work.tile([P, PASSES * P], U32, name="k_words", align_bytes=64)
+            k_scales = work.tile([P, PASSES * P], U8, name="k_scales", align_bytes=64)
+            nc.vector.quantize_mx(
+                out=k_words[:].bitcast(FP8X4),
+                scales=k_scales[:],
+                in_=k_star[:].rearrange("p g n t -> p (g n t)"),
+            )
+
+            result = work.tile([P, N_COLS], F32, name="result")
+            acc = [
+                psum_out.tile([P, BANK], F32, name="acc%d" % h, tag="acc") for h in range(HALVES)
+            ]
+            for g in range(PASSES):
+                for h in range(HALVES):
+                    nc.tensor.matmul_mx(
+                        out=acc[h][:],
+                        lhsT=k_words[:, g * P : (g + 1) * P].bitcast(FP8X4),
+                        lhsT_scale=k_scales[:, g * P : (g + 1) * P],
+                        rhs=w_words[:, g, h * BANK : (h + 1) * BANK].bitcast(FP8X4),
+                        rhs_scale=w_scales[:, g, h * BANK : (h + 1) * BANK],
+                        start=(g == 0),
+                        stop=(g == PASSES - 1),
+                    )
+            for h in range(HALVES):
+                nc.scalar.copy(out=result[:, h * BANK : (h + 1) * BANK], in_=acc[h][:])
+            nc.sync.dma_start(out=out_tiles[i], in_=result[:])

@@ -25,9 +25,13 @@ SLABS = PASSES * PACK
 N_TILES = N_ROWS // P
 BANK = 512
 HALVES = N_COLS // BANK
-VECTOR_DIMS = 6
-PAIRS = VECTOR_DIMS // 2
+VECTOR_DIMS = 5
+CHAINS = DIMS - VECTOR_DIMS + 1
 FIXED = DIMS
+SUM_LAG = 1
+WORDS_LAG = 2
+MULTIPLY_LAG = 3
+STORE_LAG = 4
 
 FLOPS = 2 * N_ROWS * M_PTS * N_COLS
 
@@ -39,6 +43,7 @@ def tile_tmgp_sg_kernel(tc, x, design_points, chol_inv_words, chol_inv_scales, o
         work = stack.enter_context(tc.tile_pool(name="work", bufs=3))
         psum_sum = stack.enter_context(tc.psum_pool(name="psum_sum", bufs=4))
         psum_out = stack.enter_context(tc.psum_pool(name="psum_out", bufs=4))
+        stack.enter_context(tc.manual_schedule())
 
         identity = const.tile([P, P], F32, name="identity")
         make_identity(nc, identity[:])
@@ -64,6 +69,12 @@ def tile_tmgp_sg_kernel(tc, x, design_points, chol_inv_words, chol_inv_scales, o
                 out=w_words[:, g, :].bitcast(I32),
                 in_=chol_inv_words[g].rearrange("p n t -> p (n t)").bitcast(I32),
             )
+
+        z32 = const.tile([P, SLABS, DIMS + 1], F32, name="z32")
+        nc.vector.tensor_copy(out=z32[:, :, 0:DIMS], in_=z_bf[:])
+        z_sum = const.tile([P, SLABS], F32, name="z_sum")
+        nc.vector.tensor_reduce(out=z_sum[:], in_=z32[:, :, 0:VECTOR_DIMS], axis=AXIS_X, op=ALU.add)
+        nc.vector.tensor_scalar_mul(out=z32[:, :, FIXED], in0=z_sum[:], scalar1=-0.5)
 
         x32 = const.tile([P, N_TILES, DIMS], F32, name="x32")
         nc.vector.tensor_copy(out=x32[:], in_=x_bf[:])
@@ -98,19 +109,11 @@ def tile_tmgp_sg_kernel(tc, x, design_points, chol_inv_words, chol_inv_scales, o
         )
         neg_half = const.tile(every_tile, F32, name="neg_half")
         nc.vector.tensor_scalar_mul(out=neg_half[:], in0=xs[:], scalar1=-0.5)
-        pair_shift = const.tile([P, N_TILES, DIMS // 2], F32, name="pair_shift")
+        shift = const.tile([P, N_TILES], F32, name="shift")
         nc.vector.tensor_reduce(
-            out=pair_shift[:],
-            in_=neg_half[:].rearrange("p i (c e) -> p i c e", e=2),
-            axis=AXIS_X,
-            op=ALU.add,
+            out=shift[:], in_=neg_half[:, :, 0:VECTOR_DIMS], axis=AXIS_X, op=ALU.add
         )
 
-        z32 = const.tile([P, SLABS, DIMS + 1], F32, name="z32")
-        nc.vector.tensor_copy(out=z32[:, :, 0:DIMS], in_=z_bf[:])
-        z_sum = const.tile([P, SLABS], F32, name="z_sum")
-        nc.vector.tensor_reduce(out=z_sum[:], in_=z32[:, :, 0:VECTOR_DIMS], axis=AXIS_X, op=ALU.add)
-        nc.vector.tensor_scalar_mul(out=z32[:, :, FIXED], in0=z_sum[:], scalar1=-0.5)
         rows = const.tile([P, DIMS + 1, M_PTS], F32, name="rows")
         for r in range(DIMS + 1):
             for g in range(PASSES):
@@ -129,89 +132,120 @@ def tile_tmgp_sg_kernel(tc, x, design_points, chol_inv_words, chol_inv_scales, o
 
         out_tiles = out.rearrange("(p i) c -> i p c", i=N_TILES)
 
-        for i in range(N_TILES):
-            pairs = []
-            for c in range(PAIRS):
-                pair = work.tile([P, M_PTS], F32, name="pair%d" % c)
-                nc.vector.tensor_scalar(
-                    out=pair[:],
-                    in0=rows[:, 2 * c, :],
-                    scalar1=xs[:, i, 2 * c : 2 * c + 1],
-                    scalar2=pair_shift[:, i, c : c + 1],
-                    op0=ALU.max,
-                    op1=ALU.add,
-                )
-                pairs.append(pair)
-            for c in range(PAIRS):
-                nc.vector.scalar_tensor_tensor(
-                    out=pairs[c][:],
-                    in0=rows[:, 2 * c + 1, :],
-                    scalar=xs[:, i, 2 * c + 1 : 2 * c + 2],
-                    in1=pairs[c][:],
-                    op0=ALU.max,
-                    op1=ALU.add,
-                )
-            singles = []
-            for d in range(VECTOR_DIMS, DIMS):
-                single = work.tile([P, M_PTS], F32, name="single%d" % d)
+        chains = {}
+        half_l1 = {}
+        k_star = {}
+        k_words = {}
+        k_scales = {}
+        acc = {}
+
+        def scalar_heads(i):
+            chains[i] = [
+                work.tile([P, M_PTS], F32, name="chain%d" % c) for c in range(CHAINS)
+            ]
+            for c in range(1, CHAINS):
+                d = VECTOR_DIMS - 1 + c
                 nc.scalar.activation(
-                    out=single[:],
+                    out=chains[i][c][:],
                     in_=rows[:, d, :],
                     func=ACT.Abs,
                     scale=0.5,
                     bias=neg_half[:, i, d : d + 1],
                 )
-                singles.append(single)
 
-            terms = [rows[:, FIXED, :]] + [s[:] for s in singles] + [q[:] for q in pairs]
-            half_l1 = [
-                psum_sum.tile([P, PACK, P], F32, name="half_l1_%d" % g, tag="bank")
-                for g in range(PASSES)
-            ]
+        def vector_terms(i):
+            nc.vector.tensor_scalar(
+                out=chains[i][0][:],
+                in0=rows[:, 0, :],
+                scalar1=xs[:, i, 0:1],
+                scalar2=shift[:, i : i + 1],
+                op0=ALU.max,
+                op1=ALU.add,
+            )
+            for c in list(range(1, CHAINS)) + [0]:
+                d = c + 1
+                nc.vector.scalar_tensor_tensor(
+                    out=chains[i][c][:],
+                    in0=rows[:, d, :],
+                    scalar=xs[:, i, d : d + 1],
+                    in1=chains[i][c][:],
+                    op0=ALU.max,
+                    op1=ALU.add,
+                )
+
+        def sum_half(i, g):
+            terms = [rows[:, FIXED, :]] + [chains[i][c][:] for c in list(range(1, CHAINS)) + [0]]
+            bank = psum_sum.tile([P, PACK, P], F32, name="half_l1", tag="bank")
+            half_l1[i, g] = bank
             for k, term in enumerate(terms):
-                for g in range(PASSES):
-                    for t in range(PACK):
-                        slab = g * PACK + t
-                        nc.tensor.matmul(
-                            out=half_l1[g][:, t, :],
-                            lhsT=term[:, slab * P : (slab + 1) * P],
-                            rhs=identity[:],
-                            is_transpose=True,
-                            start=(k == 0 and t == 0),
-                            stop=(k == len(terms) - 1 and t == PACK - 1),
-                        )
+                for t in range(PACK):
+                    slab = g * PACK + t
+                    nc.tensor.matmul(
+                        out=bank[:, t, :],
+                        lhsT=term[:, slab * P : (slab + 1) * P],
+                        rhs=identity[:],
+                        is_transpose=True,
+                        start=(k == 0 and t == 0),
+                        stop=(k == len(terms) - 1 and t == PACK - 1),
+                    )
 
-            k_star = work.tile([P, PASSES, P, PACK], BF16, name="k_star", align_bytes=64)
+        def multiply_half(i, g):
+            if g == 0:
+                acc[i] = [
+                    psum_out.tile([P, BANK], F32, name="acc%d" % h, tag="acc") for h in range(HALVES)
+                ]
+            for h in range(HALVES):
+                nc.tensor.matmul_mx(
+                    out=acc[i][h][:],
+                    lhsT=k_words[i][:, g * P : (g + 1) * P].bitcast(FP8X4),
+                    lhsT_scale=k_scales[i][:, g * P : (g + 1) * P],
+                    rhs=w_words[:, g, h * BANK : (h + 1) * BANK].bitcast(FP8X4),
+                    rhs_scale=w_scales[:, g, h * BANK : (h + 1) * BANK],
+                    start=(g == 0),
+                    stop=(g == PASSES - 1),
+                )
+
+        def exponential(i):
+            k_star[i] = work.tile([P, PASSES, P, PACK], BF16, name="k_star", align_bytes=64)
             for g in range(PASSES):
                 nc.scalar.activation(
-                    out=k_star[:, g, :, :],
-                    in_=half_l1[g][:].rearrange("p t n -> p n t"),
+                    out=k_star[i][:, g, :, :],
+                    in_=half_l1[i, g][:].rearrange("p t n -> p n t"),
                     func=ACT.Exp,
                     scale=-2.0,
                 )
-            k_words = work.tile([P, PASSES * P], U32, name="k_words", align_bytes=64)
-            k_scales = work.tile([P, PASSES * P], U8, name="k_scales", align_bytes=64)
+
+        def quantise(i):
+            k_words[i] = work.tile([P, PASSES * P], U32, name="k_words", align_bytes=64)
+            k_scales[i] = work.tile([P, PASSES * P], U8, name="k_scales", align_bytes=64)
             nc.vector.quantize_mx(
-                out=k_words[:].bitcast(FP8X4),
-                scales=k_scales[:],
-                in_=k_star[:].rearrange("p g n t -> p (g n t)"),
+                out=k_words[i][:].bitcast(FP8X4),
+                scales=k_scales[i][:],
+                in_=k_star[i][:].rearrange("p g n t -> p (g n t)"),
             )
 
+        def store(i):
             result = work.tile([P, N_COLS], F32, name="result")
-            acc = [
-                psum_out.tile([P, BANK], F32, name="acc%d" % h, tag="acc") for h in range(HALVES)
-            ]
-            for g in range(PASSES):
-                for h in range(HALVES):
-                    nc.tensor.matmul_mx(
-                        out=acc[h][:],
-                        lhsT=k_words[:, g * P : (g + 1) * P].bitcast(FP8X4),
-                        lhsT_scale=k_scales[:, g * P : (g + 1) * P],
-                        rhs=w_words[:, g, h * BANK : (h + 1) * BANK].bitcast(FP8X4),
-                        rhs_scale=w_scales[:, g, h * BANK : (h + 1) * BANK],
-                        start=(g == 0),
-                        stop=(g == PASSES - 1),
-                    )
             for h in range(HALVES):
-                nc.scalar.copy(out=result[:, h * BANK : (h + 1) * BANK], in_=acc[h][:])
+                nc.scalar.copy(out=result[:, h * BANK : (h + 1) * BANK], in_=acc[i][h][:])
             nc.sync.dma_start(out=out_tiles[i], in_=result[:])
+
+        def live(i):
+            return 0 <= i < N_TILES
+
+        scalar_heads(0)
+        for step in range(N_TILES + STORE_LAG):
+            if live(step + 1):
+                scalar_heads(step + 1)
+            if live(step):
+                vector_terms(step)
+            for g in range(PASSES):
+                if live(step - SUM_LAG):
+                    sum_half(step - SUM_LAG, g)
+                if live(step - MULTIPLY_LAG):
+                    multiply_half(step - MULTIPLY_LAG, g)
+            if live(step - WORDS_LAG):
+                exponential(step - WORDS_LAG)
+                quantise(step - WORDS_LAG)
+            if live(step - STORE_LAG):
+                store(step - STORE_LAG)

@@ -25,13 +25,11 @@ SLABS = PASSES * PACK
 N_TILES = N_ROWS // P
 BANK = 512
 HALVES = N_COLS // BANK
-VECTOR_DIMS = 5
-CHAINS = DIMS - VECTOR_DIMS + 1
+VECTOR_DIMS = 4
+MAX_DIMS = 6
 FIXED = DIMS
-SUM_LAG = 1
-WORDS_LAG = 2
-MULTIPLY_LAG = 3
-STORE_LAG = 4
+TERMS = DIMS + 1 - VECTOR_DIMS
+LARGEST = 3.4028234663852886e38
 
 FLOPS = 2 * N_ROWS * M_PTS * N_COLS
 
@@ -41,12 +39,13 @@ def tile_tmgp_sg_kernel(tc, x, design_points, chol_inv_words, chol_inv_scales, o
     with ExitStack() as stack:
         const = stack.enter_context(tc.tile_pool(name="const", bufs=1))
         work = stack.enter_context(tc.tile_pool(name="work", bufs=3))
-        psum_sum = stack.enter_context(tc.psum_pool(name="psum_sum", bufs=4))
-        psum_out = stack.enter_context(tc.psum_pool(name="psum_out", bufs=4))
+        psum = stack.enter_context(tc.psum_pool(name="psum", bufs=1))
         stack.enter_context(tc.manual_schedule())
 
         identity = const.tile([P, P], F32, name="identity")
         make_identity(nc, identity[:])
+        identity_bf = const.tile([P, P], BF16, name="identity_bf")
+        make_identity(nc, identity_bf[:])
 
         x_bf = const.tile([P, N_TILES, DIMS], BF16, name="x_bf")
         nc.sync.dma_start(out=x_bf[:], in_=x.rearrange("(p i) d -> p i d", i=N_TILES))
@@ -73,7 +72,7 @@ def tile_tmgp_sg_kernel(tc, x, design_points, chol_inv_words, chol_inv_scales, o
         z32 = const.tile([P, SLABS, DIMS + 1], F32, name="z32")
         nc.vector.tensor_copy(out=z32[:, :, 0:DIMS], in_=z_bf[:])
         z_sum = const.tile([P, SLABS], F32, name="z_sum")
-        nc.vector.tensor_reduce(out=z_sum[:], in_=z32[:, :, 0:VECTOR_DIMS], axis=AXIS_X, op=ALU.add)
+        nc.vector.tensor_reduce(out=z_sum[:], in_=z32[:, :, 0:MAX_DIMS], axis=AXIS_X, op=ALU.add)
         nc.vector.tensor_scalar_mul(out=z32[:, :, FIXED], in0=z_sum[:], scalar1=-0.5)
 
         x32 = const.tile([P, N_TILES, DIMS], F32, name="x32")
@@ -85,11 +84,11 @@ def tile_tmgp_sg_kernel(tc, x, design_points, chol_inv_words, chol_inv_scales, o
         lowest = const.tile([P, DIMS], F32, name="lowest")
         nc.vector.tensor_reduce(out=lowest[:], in_=by_dim, axis=AXIS_X, op=ALU.min)
         nc.vector.tensor_scalar_mul(out=own[:, DIMS : 2 * DIMS], in0=lowest[:], scalar1=-1.0)
-        own_t = psum_sum.tile([P, P], F32, name="own_t", tag="bank")
+        own_t = psum.tile([P, P], F32, name="own_t", tag="sum0")
         nc.tensor.transpose(out=own_t[:], in_=own[:], identity=identity[:])
         overall = const.tile([P, 1], F32, name="overall")
         nc.vector.tensor_reduce(out=overall[:], in_=own_t[:], axis=AXIS_X, op=ALU.max)
-        overall_t = psum_sum.tile([P, P], F32, name="overall_t", tag="bank")
+        overall_t = psum.tile([P, P], F32, name="overall_t", tag="sum1")
         nc.tensor.transpose(
             out=overall_t[:], in_=overall[:, 0:1].to_broadcast([P, P]), identity=identity[:]
         )
@@ -111,109 +110,113 @@ def tile_tmgp_sg_kernel(tc, x, design_points, chol_inv_words, chol_inv_scales, o
         nc.vector.tensor_scalar_mul(out=neg_half[:], in0=xs[:], scalar1=-0.5)
         shift = const.tile([P, N_TILES], F32, name="shift")
         nc.vector.tensor_reduce(
-            out=shift[:], in_=neg_half[:, :, 0:VECTOR_DIMS], axis=AXIS_X, op=ALU.add
+            out=shift[:], in_=neg_half[:, :, 0:MAX_DIMS], axis=AXIS_X, op=ALU.add
         )
 
-        rows = const.tile([P, DIMS + 1, M_PTS], F32, name="rows")
-        for r in range(DIMS + 1):
+        rows = const.tile([P, TERMS, M_PTS], F32, name="rows")
+        for k in range(TERMS):
+            column = FIXED if k == 0 else VECTOR_DIMS + k - 1
             for g in range(PASSES):
-                spread = psum_sum.tile([P, PACK, P], F32, name="spread", tag="bank")
+                bank_tag = ("sum%d" if k % 2 == 0 else "acc%d") % g
+                spread = psum.tile([P, PACK, P], F32, name="spread", tag=bank_tag)
                 for t in range(PACK):
                     nc.tensor.transpose(
                         out=spread[:, t, :],
-                        in_=z32[:, g * PACK + t, r : r + 1].to_broadcast([P, P]),
+                        in_=z32[:, g * PACK + t, column : column + 1].to_broadcast([P, P]),
                         identity=identity[:],
                     )
-                half_row = rows[:, r, g * K_PASS : (g + 1) * K_PASS]
+                half_row = rows[:, k, g * K_PASS : (g + 1) * K_PASS]
                 if g == 0:
                     nc.vector.tensor_copy(out=half_row, in_=spread[:].rearrange("p t q -> p (t q)"))
                 else:
                     nc.scalar.copy(out=half_row, in_=spread[:].rearrange("p t q -> p (t q)"))
 
+        z_rows = [psum.tile([P, M_PTS], BF16, name="z_row%d" % d) for d in range(VECTOR_DIMS)]
+        for d in range(VECTOR_DIMS):
+            for s in range(SLABS):
+                nc.tensor.transpose(
+                    out=z_rows[d][:, s * P : (s + 1) * P],
+                    in_=z_bf[:, s, d : d + 1].to_broadcast([P, P]),
+                    identity=identity_bf[:],
+                )
+
         out_tiles = out.rearrange("(p i) c -> i p c", i=N_TILES)
 
-        chains = {}
+        terms = {}
         half_l1 = {}
         k_star = {}
         k_words = {}
         k_scales = {}
         acc = {}
+        result = {}
 
-        def scalar_heads(i):
-            chains[i] = [
-                work.tile([P, M_PTS], F32, name="chain%d" % c) for c in range(CHAINS)
-            ]
-            for c in range(1, CHAINS):
-                d = VECTOR_DIMS - 1 + c
-                nc.scalar.activation(
-                    out=chains[i][c][:],
-                    in_=rows[:, d, :],
-                    func=ACT.Abs,
-                    scale=0.5,
-                    bias=neg_half[:, i, d : d + 1],
-                )
-
-        def vector_terms(i):
-            nc.vector.tensor_scalar(
-                out=chains[i][0][:],
+        def gpsimd_heads(i):
+            terms[i] = [work.tile([P, M_PTS], F32, name="term%d" % k) for k in range(TERMS)]
+            nc.gpsimd.tensor_scalar(
+                out=terms[i][0][:],
                 in0=rows[:, 0, :],
-                scalar1=xs[:, i, 0:1],
+                scalar1=1.0,
                 scalar2=shift[:, i : i + 1],
-                op0=ALU.max,
+                op0=ALU.mult,
                 op1=ALU.add,
             )
-            for c in list(range(1, CHAINS)) + [0]:
-                d = c + 1
+            for d in range(VECTOR_DIMS, MAX_DIMS):
+                k = d - VECTOR_DIMS + 1
+                nc.gpsimd.tensor_scalar(
+                    out=terms[i][k][:],
+                    in0=rows[:, k, :],
+                    scalar1=LARGEST,
+                    scalar2=xs[:, i, d : d + 1],
+                    op0=ALU.min,
+                    op1=ALU.max,
+                )
+
+        def scalar_head(i, d):
+            k = d - VECTOR_DIMS + 1
+            nc.scalar.activation(
+                out=terms[i][k][:],
+                in_=rows[:, k, :],
+                func=ACT.Abs,
+                scale=0.5,
+                bias=neg_half[:, i, d : d + 1],
+            )
+
+        def vector_terms(i):
+            for k in range(VECTOR_DIMS):
                 nc.vector.scalar_tensor_tensor(
-                    out=chains[i][c][:],
-                    in0=rows[:, d, :],
-                    scalar=xs[:, i, d : d + 1],
-                    in1=chains[i][c][:],
+                    out=terms[i][k][:],
+                    in0=z_rows[k][:],
+                    scalar=xs[:, i, k : k + 1],
+                    in1=terms[i][k][:],
                     op0=ALU.max,
                     op1=ALU.add,
                 )
 
         def sum_half(i, g):
-            terms = [rows[:, FIXED, :]] + [chains[i][c][:] for c in list(range(1, CHAINS)) + [0]]
-            bank = psum_sum.tile([P, PACK, P], F32, name="half_l1", tag="bank")
+            bank = psum.tile([P, PACK, P], F32, name="half_l1", tag="sum%d" % g)
             half_l1[i, g] = bank
-            for k, term in enumerate(terms):
+            order = [TERMS - 1] + list(range(VECTOR_DIMS))
+            for place, k in enumerate(order):
                 for t in range(PACK):
                     slab = g * PACK + t
                     nc.tensor.matmul(
                         out=bank[:, t, :],
-                        lhsT=term[:, slab * P : (slab + 1) * P],
+                        lhsT=terms[i][k][:, slab * P : (slab + 1) * P],
                         rhs=identity[:],
                         is_transpose=True,
-                        start=(k == 0 and t == 0),
-                        stop=(k == len(terms) - 1 and t == PACK - 1),
+                        start=(place == 0 and t == 0),
+                        stop=(place == TERMS - 1 and t == PACK - 1),
                     )
 
-        def multiply_half(i, g):
+        def exponential(i, g):
             if g == 0:
-                acc[i] = [
-                    psum_out.tile([P, BANK], F32, name="acc%d" % h, tag="acc") for h in range(HALVES)
-                ]
-            for h in range(HALVES):
-                nc.tensor.matmul_mx(
-                    out=acc[i][h][:],
-                    lhsT=k_words[i][:, g * P : (g + 1) * P].bitcast(FP8X4),
-                    lhsT_scale=k_scales[i][:, g * P : (g + 1) * P],
-                    rhs=w_words[:, g, h * BANK : (h + 1) * BANK].bitcast(FP8X4),
-                    rhs_scale=w_scales[:, g, h * BANK : (h + 1) * BANK],
-                    start=(g == 0),
-                    stop=(g == PASSES - 1),
-                )
-
-        def exponential(i):
-            k_star[i] = work.tile([P, PASSES, P, PACK], BF16, name="k_star", align_bytes=64)
-            for g in range(PASSES):
-                nc.scalar.activation(
-                    out=k_star[i][:, g, :, :],
-                    in_=half_l1[i, g][:].rearrange("p t n -> p n t"),
-                    func=ACT.Exp,
-                    scale=-2.0,
-                )
+                k_star[i] = work.tile([P, PASSES, P, PACK], BF16, name="k_star", align_bytes=64)
+            nc.scalar.activation(
+                out=k_star[i][:, g, :, :],
+                in_=half_l1[i, g][:].rearrange("p t n -> p n t"),
+                func=ACT.Exp,
+                scale=-2.0,
+            )
 
         def quantise(i):
             k_words[i] = work.tile([P, PASSES * P], U32, name="k_words", align_bytes=64)
@@ -224,28 +227,49 @@ def tile_tmgp_sg_kernel(tc, x, design_points, chol_inv_words, chol_inv_scales, o
                 in_=k_star[i][:].rearrange("p g n t -> p (g n t)"),
             )
 
-        def store(i):
-            result = work.tile([P, N_COLS], F32, name="result")
-            for h in range(HALVES):
-                nc.scalar.copy(out=result[:, h * BANK : (h + 1) * BANK], in_=acc[i][h][:])
-            nc.sync.dma_start(out=out_tiles[i], in_=result[:])
+        def multiply(i, h):
+            acc[i, h] = psum.tile([P, BANK], F32, name="acc", tag="acc%d" % h)
+            for g in range(PASSES):
+                nc.tensor.matmul_mx(
+                    out=acc[i, h][:],
+                    lhsT=k_words[i][:, g * P : (g + 1) * P].bitcast(FP8X4),
+                    lhsT_scale=k_scales[i][:, g * P : (g + 1) * P],
+                    rhs=w_words[:, g, h * BANK : (h + 1) * BANK].bitcast(FP8X4),
+                    rhs_scale=w_scales[:, g, h * BANK : (h + 1) * BANK],
+                    start=(g == 0),
+                    stop=(g == PASSES - 1),
+                )
+
+        def copy_out(i, h):
+            if h == 0:
+                result[i] = work.tile([P, N_COLS], F32, name="result")
+            nc.scalar.copy(out=result[i][:, h * BANK : (h + 1) * BANK], in_=acc[i, h][:])
+            if h == HALVES - 1:
+                nc.sync.dma_start(out=out_tiles[i], in_=result[i][:])
 
         def live(i):
             return 0 <= i < N_TILES
 
-        scalar_heads(0)
-        for step in range(N_TILES + STORE_LAG):
+        gpsimd_heads(0)
+        for d in range(MAX_DIMS, DIMS):
+            scalar_head(0, d)
+        for step in range(N_TILES + 3):
+            if live(step - 2):
+                quantise(step - 2)
             if live(step + 1):
-                scalar_heads(step + 1)
+                gpsimd_heads(step + 1)
+            for half in range(2):
+                if half == 0 and live(step - 3):
+                    copy_out(step - 3, 1)
+                if half == 1 and live(step - 2):
+                    copy_out(step - 2, 0)
+                if live(step + 1):
+                    scalar_head(step + 1, MAX_DIMS + half)
+                if live(step - 1):
+                    sum_half(step - 1, half)
+                if live(step - 2):
+                    multiply(step - 2, half)
+                if live(step - 1):
+                    exponential(step - 1, half)
             if live(step):
                 vector_terms(step)
-            for g in range(PASSES):
-                if live(step - SUM_LAG):
-                    sum_half(step - SUM_LAG, g)
-                if live(step - MULTIPLY_LAG):
-                    multiply_half(step - MULTIPLY_LAG, g)
-            if live(step - WORDS_LAG):
-                exponential(step - WORDS_LAG)
-                quantise(step - WORDS_LAG)
-            if live(step - STORE_LAG):
-                store(step - STORE_LAG)

@@ -29,6 +29,7 @@ VECTOR_DIMS = 4
 MAX_DIMS = 6
 FIXED = DIMS
 TERMS = DIMS + 1 - VECTOR_DIMS
+TERM_ORDER = (2, 3, 4, 1)
 LARGEST = 3.4028234663852886e38
 
 FLOPS = 2 * N_ROWS * M_PTS * N_COLS
@@ -68,6 +69,15 @@ def tile_tmgp_sg_kernel(tc, x, design_points, chol_inv_words, chol_inv_scales, o
                 out=w_words[:, g, :].bitcast(I32),
                 in_=chol_inv_words[g].rearrange("p n t -> p (n t)").bitcast(I32),
             )
+
+        z_rows = [psum.tile([P, M_PTS], BF16, name="z_row%d" % d) for d in range(VECTOR_DIMS)]
+        for d in range(VECTOR_DIMS):
+            for s in range(SLABS):
+                nc.tensor.transpose(
+                    out=z_rows[d][:, s * P : (s + 1) * P],
+                    in_=z_bf[:, s, d : d + 1].to_broadcast([P, P]),
+                    identity=identity_bf[:],
+                )
 
         z32 = const.tile([P, SLABS, DIMS + 1], F32, name="z32")
         nc.vector.tensor_copy(out=z32[:, :, 0:DIMS], in_=z_bf[:])
@@ -113,12 +123,21 @@ def tile_tmgp_sg_kernel(tc, x, design_points, chol_inv_words, chol_inv_scales, o
             out=shift[:], in_=neg_half[:, :, 0:MAX_DIMS], axis=AXIS_X, op=ALU.add
         )
 
+        out_tiles = out.rearrange("(p i) c -> i p c", i=N_TILES)
         rows = const.tile([P, TERMS, M_PTS], F32, name="rows")
-        for k in range(TERMS):
+
+        terms = {}
+        half_l1 = {}
+        k_star = {}
+        k_words = {}
+        k_scales = {}
+        acc = {}
+        result = {}
+
+        def build_row(k, bank_kind):
             column = FIXED if k == 0 else VECTOR_DIMS + k - 1
             for g in range(PASSES):
-                bank_tag = ("sum%d" if k % 2 == 0 else "acc%d") % g
-                spread = psum.tile([P, PACK, P], F32, name="spread", tag=bank_tag)
+                spread = psum.tile([P, PACK, P], F32, name="spread", tag=bank_kind % g)
                 for t in range(PACK):
                     nc.tensor.transpose(
                         out=spread[:, t, :],
@@ -131,77 +150,58 @@ def tile_tmgp_sg_kernel(tc, x, design_points, chol_inv_words, chol_inv_scales, o
                 else:
                     nc.scalar.copy(out=half_row, in_=spread[:].rearrange("p t q -> p (t q)"))
 
-        z_rows = [psum.tile([P, M_PTS], BF16, name="z_row%d" % d) for d in range(VECTOR_DIMS)]
-        for d in range(VECTOR_DIMS):
-            for s in range(SLABS):
-                nc.tensor.transpose(
-                    out=z_rows[d][:, s * P : (s + 1) * P],
-                    in_=z_bf[:, s, d : d + 1].to_broadcast([P, P]),
-                    identity=identity_bf[:],
+        def start_term(i, k):
+            d = VECTOR_DIMS + k - 1
+            term = work.tile([P, M_PTS], F32, name="term%d" % k)
+            terms[i, k] = term
+            if k == 1:
+                nc.vector.tensor_scalar(
+                    out=term[:],
+                    in0=rows[:, k, :],
+                    scalar1=xs[:, i, d : d + 1],
+                    scalar2=shift[:, i : i + 1],
+                    op0=ALU.max,
+                    op1=ALU.add,
                 )
-
-        out_tiles = out.rearrange("(p i) c -> i p c", i=N_TILES)
-
-        terms = {}
-        half_l1 = {}
-        k_star = {}
-        k_words = {}
-        k_scales = {}
-        acc = {}
-        result = {}
-
-        def gpsimd_heads(i):
-            terms[i] = [work.tile([P, M_PTS], F32, name="term%d" % k) for k in range(TERMS)]
-            nc.gpsimd.tensor_scalar(
-                out=terms[i][0][:],
-                in0=rows[:, 0, :],
-                scalar1=1.0,
-                scalar2=shift[:, i : i + 1],
-                op0=ALU.mult,
-                op1=ALU.add,
-            )
-            for d in range(VECTOR_DIMS, MAX_DIMS):
-                k = d - VECTOR_DIMS + 1
+            elif k == 2:
                 nc.gpsimd.tensor_scalar(
-                    out=terms[i][k][:],
+                    out=term[:],
                     in0=rows[:, k, :],
                     scalar1=LARGEST,
                     scalar2=xs[:, i, d : d + 1],
                     op0=ALU.min,
                     op1=ALU.max,
                 )
-
-        def scalar_head(i, d):
-            k = d - VECTOR_DIMS + 1
-            nc.scalar.activation(
-                out=terms[i][k][:],
-                in_=rows[:, k, :],
-                func=ACT.Abs,
-                scale=0.5,
-                bias=neg_half[:, i, d : d + 1],
-            )
-
-        def vector_terms(i):
-            for k in range(VECTOR_DIMS):
-                nc.vector.scalar_tensor_tensor(
-                    out=terms[i][k][:],
-                    in0=z_rows[k][:],
-                    scalar=xs[:, i, k : k + 1],
-                    in1=terms[i][k][:],
-                    op0=ALU.max,
-                    op1=ALU.add,
+            else:
+                nc.scalar.activation(
+                    out=term[:],
+                    in_=rows[:, k, :],
+                    func=ACT.Abs,
+                    scale=0.5,
+                    bias=neg_half[:, i, d : d + 1],
                 )
+
+        def extend_term(i, k):
+            d = k - 1
+            nc.vector.scalar_tensor_tensor(
+                out=terms[i, k][:],
+                in0=z_rows[d][:],
+                scalar=xs[:, i, d : d + 1],
+                in1=terms[i, k][:],
+                op0=ALU.max,
+                op1=ALU.add,
+            )
 
         def sum_half(i, g):
             bank = psum.tile([P, PACK, P], F32, name="half_l1", tag="sum%d" % g)
             half_l1[i, g] = bank
-            order = [TERMS - 1] + list(range(VECTOR_DIMS))
-            for place, k in enumerate(order):
+            sources = [rows[:, 0, :]] + [terms[i, k][:] for k in TERM_ORDER]
+            for place, source in enumerate(sources):
                 for t in range(PACK):
                     slab = g * PACK + t
                     nc.tensor.matmul(
                         out=bank[:, t, :],
-                        lhsT=terms[i][k][:, slab * P : (slab + 1) * P],
+                        lhsT=source[:, slab * P : (slab + 1) * P],
                         rhs=identity[:],
                         is_transpose=True,
                         start=(place == 0 and t == 0),
@@ -250,26 +250,34 @@ def tile_tmgp_sg_kernel(tc, x, design_points, chol_inv_words, chol_inv_scales, o
         def live(i):
             return 0 <= i < N_TILES
 
-        gpsimd_heads(0)
-        for d in range(MAX_DIMS, DIMS):
-            scalar_head(0, d)
+        previous = None
+        for place, k in enumerate(TERM_ORDER + (0,)):
+            build_row(k, "sum%d" if place % 2 == 0 else "acc%d")
+            if k != 0:
+                start_term(0, k)
+            if previous is not None:
+                extend_term(0, previous)
+            previous = k
+
         for step in range(N_TILES + 3):
             if live(step - 2):
                 quantise(step - 2)
             if live(step + 1):
-                gpsimd_heads(step + 1)
+                start_term(step + 1, 2)
             for half in range(2):
                 if half == 0 and live(step - 3):
                     copy_out(step - 3, 1)
                 if half == 1 and live(step - 2):
                     copy_out(step - 2, 0)
                 if live(step + 1):
-                    scalar_head(step + 1, MAX_DIMS + half)
+                    start_term(step + 1, 3 + half)
                 if live(step - 1):
                     sum_half(step - 1, half)
                 if live(step - 2):
                     multiply(step - 2, half)
                 if live(step - 1):
                     exponential(step - 1, half)
-            if live(step):
-                vector_terms(step)
+            if live(step) and step > 0:
+                start_term(step, 1)
+                for k in TERM_ORDER:
+                    extend_term(step, k)

@@ -27,8 +27,7 @@ BANK = 512
 HALVES = N_COLS // BANK
 VECTOR_DIMS = 4
 MAX_DIMS = 6
-FIXED = DIMS
-TERMS = DIMS + 1 - VECTOR_DIMS
+TERMS = DIMS - VECTOR_DIMS
 TERM_ORDER = (2, 3, 4, 1)
 LARGEST = 3.4028234663852886e38
 
@@ -40,6 +39,7 @@ def tile_tmgp_sg_kernel(tc, x, design_points, chol_inv_words, chol_inv_scales, o
     with ExitStack() as stack:
         const = stack.enter_context(tc.tile_pool(name="const", bufs=1))
         work = stack.enter_context(tc.tile_pool(name="work", bufs=3))
+        single = stack.enter_context(tc.tile_pool(name="single", bufs=1))
         psum = stack.enter_context(tc.psum_pool(name="psum", bufs=1))
         stack.enter_context(tc.manual_schedule())
 
@@ -79,11 +79,10 @@ def tile_tmgp_sg_kernel(tc, x, design_points, chol_inv_words, chol_inv_scales, o
                     identity=identity_bf[:],
                 )
 
-        z32 = const.tile([P, SLABS, DIMS + 1], F32, name="z32")
-        nc.vector.tensor_copy(out=z32[:, :, 0:DIMS], in_=z_bf[:])
+        z32 = const.tile([P, SLABS, DIMS], F32, name="z32")
+        nc.vector.tensor_copy(out=z32[:], in_=z_bf[:])
         z_sum = const.tile([P, SLABS], F32, name="z_sum")
         nc.vector.tensor_reduce(out=z_sum[:], in_=z32[:, :, 0:MAX_DIMS], axis=AXIS_X, op=ALU.add)
-        nc.vector.tensor_scalar_mul(out=z32[:, :, FIXED], in0=z_sum[:], scalar1=-0.5)
 
         x32 = const.tile([P, N_TILES, DIMS], F32, name="x32")
         nc.vector.tensor_copy(out=x32[:], in_=x_bf[:])
@@ -128,6 +127,7 @@ def tile_tmgp_sg_kernel(tc, x, design_points, chol_inv_words, chol_inv_scales, o
 
         terms = {}
         half_l1 = {}
+        planar = {}
         k_star = {}
         k_words = {}
         k_scales = {}
@@ -135,7 +135,7 @@ def tile_tmgp_sg_kernel(tc, x, design_points, chol_inv_words, chol_inv_scales, o
         result = {}
 
         def build_row(k, bank_kind):
-            column = FIXED if k == 0 else VECTOR_DIMS + k - 1
+            column = VECTOR_DIMS + k - 1
             for g in range(PASSES):
                 spread = psum.tile([P, PACK, P], F32, name="spread", tag=bank_kind % g)
                 for t in range(PACK):
@@ -144,7 +144,7 @@ def tile_tmgp_sg_kernel(tc, x, design_points, chol_inv_words, chol_inv_scales, o
                         in_=z32[:, g * PACK + t, column : column + 1].to_broadcast([P, P]),
                         identity=identity[:],
                     )
-                half_row = rows[:, k, g * K_PASS : (g + 1) * K_PASS]
+                half_row = rows[:, k - 1, g * K_PASS : (g + 1) * K_PASS]
                 if g == 0:
                     nc.vector.tensor_copy(out=half_row, in_=spread[:].rearrange("p t q -> p (t q)"))
                 else:
@@ -157,7 +157,7 @@ def tile_tmgp_sg_kernel(tc, x, design_points, chol_inv_words, chol_inv_scales, o
             if k == 1:
                 nc.vector.tensor_scalar(
                     out=term[:],
-                    in0=rows[:, k, :],
+                    in0=rows[:, k - 1, :],
                     scalar1=xs[:, i, d : d + 1],
                     scalar2=shift[:, i : i + 1],
                     op0=ALU.max,
@@ -166,7 +166,7 @@ def tile_tmgp_sg_kernel(tc, x, design_points, chol_inv_words, chol_inv_scales, o
             elif k == 2:
                 nc.gpsimd.tensor_scalar(
                     out=term[:],
-                    in0=rows[:, k, :],
+                    in0=rows[:, k - 1, :],
                     scalar1=LARGEST,
                     scalar2=xs[:, i, d : d + 1],
                     op0=ALU.min,
@@ -175,7 +175,7 @@ def tile_tmgp_sg_kernel(tc, x, design_points, chol_inv_words, chol_inv_scales, o
             else:
                 nc.scalar.activation(
                     out=term[:],
-                    in_=rows[:, k, :],
+                    in_=rows[:, k - 1, :],
                     func=ACT.Abs,
                     scale=0.5,
                     bias=neg_half[:, i, d : d + 1],
@@ -195,7 +195,7 @@ def tile_tmgp_sg_kernel(tc, x, design_points, chol_inv_words, chol_inv_scales, o
         def sum_half(i, g):
             bank = psum.tile([P, PACK, P], F32, name="half_l1", tag="sum%d" % g)
             half_l1[i, g] = bank
-            sources = [rows[:, 0, :]] + [terms[i, k][:] for k in TERM_ORDER]
+            sources = [terms[i, k][:] for k in TERM_ORDER]
             for place, source in enumerate(sources):
                 for t in range(PACK):
                     slab = g * PACK + t
@@ -210,12 +210,26 @@ def tile_tmgp_sg_kernel(tc, x, design_points, chol_inv_words, chol_inv_scales, o
 
         def exponential(i, g):
             if g == 0:
-                k_star[i] = work.tile([P, PASSES, P, PACK], BF16, name="k_star", align_bytes=64)
-            nc.scalar.activation(
-                out=k_star[i][:, g, :, :],
-                in_=half_l1[i, g][:].rearrange("p t n -> p n t"),
-                func=ACT.Exp,
-                scale=-2.0,
+                planar[i] = work.tile([P, PASSES, PACK, P], BF16, name="planar")
+            for t in range(PACK):
+                slab = g * PACK + t
+                nc.scalar.activation(
+                    out=planar[i][:, g, t, :],
+                    in_=half_l1[i, g][:, t, :],
+                    func=ACT.Exp,
+                    scale=-2.0,
+                    bias=z_sum[:, slab : slab + 1],
+                )
+
+        def interleave(i):
+            k_star[i] = single.tile([P, PASSES, P, PACK], BF16, name="k_star", align_bytes=64)
+            nc.gpsimd.tensor_scalar(
+                out=k_star[i][:],
+                in0=planar[i][:].rearrange("p g t n -> p g n t"),
+                scalar1=1.0,
+                scalar2=0.0,
+                op0=ALU.mult,
+                op1=ALU.add,
             )
 
         def quantise(i):
@@ -251,30 +265,32 @@ def tile_tmgp_sg_kernel(tc, x, design_points, chol_inv_words, chol_inv_scales, o
             return 0 <= i < N_TILES
 
         previous = None
-        for place, k in enumerate(TERM_ORDER + (0,)):
+        for place, k in enumerate(TERM_ORDER):
             build_row(k, "sum%d" if place % 2 == 0 else "acc%d")
-            if k != 0:
-                start_term(0, k)
+            start_term(0, k)
             if previous is not None:
                 extend_term(0, previous)
             previous = k
+        extend_term(0, previous)
 
-        for step in range(N_TILES + 3):
+        for step in range(N_TILES + 4):
+            if live(step - 3):
+                quantise(step - 3)
             if live(step - 2):
-                quantise(step - 2)
+                interleave(step - 2)
             if live(step + 1):
                 start_term(step + 1, 2)
             for half in range(2):
-                if half == 0 and live(step - 3):
-                    copy_out(step - 3, 1)
-                if half == 1 and live(step - 2):
-                    copy_out(step - 2, 0)
+                if half == 0 and live(step - 4):
+                    copy_out(step - 4, 1)
+                if half == 1 and live(step - 3):
+                    copy_out(step - 3, 0)
                 if live(step + 1):
                     start_term(step + 1, 3 + half)
                 if live(step - 1):
                     sum_half(step - 1, half)
-                if live(step - 2):
-                    multiply(step - 2, half)
+                if live(step - 3):
+                    multiply(step - 3, half)
                 if live(step - 1):
                     exponential(step - 1, half)
             if live(step) and step > 0:

@@ -29,6 +29,8 @@ VECTOR_DIMS = 4
 MAX_DIMS = 6
 TERMS = DIMS - VECTOR_DIMS
 TERM_ORDER = (2, 3, 4, 1)
+SHARED = VECTOR_DIMS - 1
+VECTOR_SLABS = PACK - 1
 LARGEST = 3.4028234663852886e38
 
 FLOPS = 2 * N_ROWS * M_PTS * N_COLS
@@ -124,6 +126,7 @@ def tile_tmgp_sg_kernel(tc, x, design_points, chol_inv_words, chol_inv_scales, o
 
         out_tiles = out.rearrange("(p i) c -> i p c", i=N_TILES)
         rows = const.tile([P, TERMS, M_PTS], F32, name="rows")
+        shared_row = const.tile([P, PASSES, P], F32, name="shared_row")
 
         terms = {}
         half_l1 = {}
@@ -183,13 +186,26 @@ def tile_tmgp_sg_kernel(tc, x, design_points, chol_inv_words, chol_inv_scales, o
 
         def extend_term(i, k):
             d = k - 1
+            width = VECTOR_SLABS * P if d == SHARED else K_PASS
+            term = terms[i, k][:].rearrange("p (g c) -> p g c", g=PASSES)[:, :, 0:width]
             nc.vector.scalar_tensor_tensor(
-                out=terms[i, k][:],
-                in0=z_rows[d][:],
+                out=term,
+                in0=z_rows[d][:].rearrange("p (g c) -> p g c", g=PASSES)[:, :, 0:width],
                 scalar=xs[:, i, d : d + 1],
-                in1=terms[i, k][:],
+                in1=term,
                 op0=ALU.max,
                 op1=ALU.add,
+            )
+
+        def start_shared(i):
+            terms[i, 0] = work.tile([P, PASSES, P], F32, name="term0")
+            nc.gpsimd.tensor_scalar(
+                out=terms[i, 0][:],
+                in0=shared_row[:],
+                scalar1=LARGEST,
+                scalar2=xs[:, i, SHARED : SHARED + 1],
+                op0=ALU.min,
+                op1=ALU.max,
             )
 
         def sum_half(i, g):
@@ -205,8 +221,16 @@ def tile_tmgp_sg_kernel(tc, x, design_points, chol_inv_words, chol_inv_scales, o
                         rhs=identity[:],
                         is_transpose=True,
                         start=(place == 0 and t == 0),
-                        stop=(place == TERMS - 1 and t == PACK - 1),
+                        stop=False,
                     )
+            nc.tensor.matmul(
+                out=bank[:, PACK - 1, :],
+                lhsT=terms[i, 0][:, g, :],
+                rhs=identity[:],
+                is_transpose=True,
+                start=False,
+                stop=True,
+            )
 
         def exponential(i, g):
             if g == 0:
@@ -264,6 +288,15 @@ def tile_tmgp_sg_kernel(tc, x, design_points, chol_inv_words, chol_inv_scales, o
         def live(i):
             return 0 <= i < N_TILES
 
+        spread_shared = psum.tile([P, PASSES, P], F32, name="spread_shared", tag="acc1")
+        for g in range(PASSES):
+            nc.tensor.transpose(
+                out=spread_shared[:, g, :],
+                in_=z32[:, g * PACK + PACK - 1, SHARED : SHARED + 1].to_broadcast([P, P]),
+                identity=identity[:],
+            )
+        nc.scalar.copy(out=shared_row[:], in_=spread_shared[:])
+        start_shared(0)
         previous = None
         for place, k in enumerate(TERM_ORDER):
             build_row(k, "sum%d" if place % 2 == 0 else "acc%d")
@@ -280,6 +313,7 @@ def tile_tmgp_sg_kernel(tc, x, design_points, chol_inv_words, chol_inv_scales, o
                 interleave(step - 2)
             if live(step + 1):
                 start_term(step + 1, 2)
+                start_shared(step + 1)
             for half in range(2):
                 if half == 0 and live(step - 4):
                     copy_out(step - 4, 1)

@@ -29,6 +29,7 @@ VECTOR_DIMS = 4
 MAX_DIMS = 6
 TERMS = DIMS - VECTOR_DIMS
 TERM_ORDER = (2, 3, 4, 1)
+BOTH = (0, 1)
 SHARED = VECTOR_DIMS - 1
 VECTOR_SLABS = PACK - 1
 LARGEST = 3.4028234663852886e38
@@ -49,6 +50,11 @@ def tile_tmgp_sg_kernel(tc, x, design_points, chol_inv_words, chol_inv_scales, o
         make_identity(nc, identity[:])
         identity_bf = const.tile([P, P], BF16, name="identity_bf")
         make_identity(nc, identity_bf[:])
+
+        zero = const.tile([P, 1], F32, name="zero")
+        nc.vector.memset(zero[:], 0.0)
+        warm = const.tile([P, 1], F32, name="warm")
+        nc.scalar.activation(out=warm[:], in_=zero[:], func=ACT.Exp)
 
         x_bf = const.tile([P, N_TILES, DIMS], BF16, name="x_bf")
         nc.sync.dma_start(out=x_bf[:], in_=x.rearrange("(p i) d -> p i d", i=N_TILES))
@@ -72,37 +78,56 @@ def tile_tmgp_sg_kernel(tc, x, design_points, chol_inv_words, chol_inv_scales, o
                 in_=chol_inv_words[g].rearrange("p n t -> p (n t)").bitcast(I32),
             )
 
-        z_rows = [psum.tile([P, M_PTS], BF16, name="z_row%d" % d) for d in range(VECTOR_DIMS)]
-        for d in range(VECTOR_DIMS):
-            for s in range(SLABS):
+        def spread(bank, d, slabs):
+            for s in slabs:
                 nc.tensor.transpose(
-                    out=z_rows[d][:, s * P : (s + 1) * P],
+                    out=bank[:, s * P : (s + 1) * P],
                     in_=z_bf[:, s, d : d + 1].to_broadcast([P, P]),
                     identity=identity_bf[:],
                 )
 
-        z32 = const.tile([P, SLABS, DIMS], F32, name="z32")
-        nc.vector.tensor_copy(out=z32[:], in_=z_bf[:])
-        z_sum = const.tile([P, SLABS], F32, name="z_sum")
-        nc.vector.tensor_reduce(out=z_sum[:], in_=z32[:, :, 0:MAX_DIMS], axis=AXIS_X, op=ALU.add)
+        rows = const.tile([P, TERMS, M_PTS], BF16, name="rows")
 
-        x32 = const.tile([P, N_TILES, DIMS], F32, name="x32")
-        nc.vector.tensor_copy(out=x32[:], in_=x_bf[:])
+        def open_row(k, tag):
+            return psum.tile([P, M_PTS], BF16, name="row", tag=tag)
+
+        def keep_row(k, bank):
+            nc.scalar.copy(out=rows[:, k - 1, :], in_=bank[:])
+
         own = const.tile([P, P], F32, name="own")
         nc.vector.memset(own[:], 0.0)
-        by_dim = x32[:].rearrange("p i d -> p d i")
+        by_dim = x_bf[:].rearrange("p i d -> p d i")
         nc.vector.tensor_reduce(out=own[:, 0:DIMS], in_=by_dim, axis=AXIS_X, op=ALU.max)
         lowest = const.tile([P, DIMS], F32, name="lowest")
         nc.vector.tensor_reduce(out=lowest[:], in_=by_dim, axis=AXIS_X, op=ALU.min)
         nc.vector.tensor_scalar_mul(out=own[:, DIMS : 2 * DIMS], in0=lowest[:], scalar1=-1.0)
-        own_t = psum.tile([P, P], F32, name="own_t", tag="sum0")
+        x32 = const.tile([P, N_TILES, DIMS], F32, name="x32")
+        nc.vector.tensor_copy(out=x32[:], in_=x_bf[:])
+        z_sum = const.tile([P, SLABS], F32, name="z_sum")
+        nc.vector.tensor_reduce(out=z_sum[:], in_=z_bf[:, :, 0:MAX_DIMS], axis=AXIS_X, op=ALU.add)
+
+        bank2 = open_row(2, "sum0")
+        spread(bank2, VECTOR_DIMS + 1, range(SLABS))
+        keep_row(2, bank2)
+        own_t = psum.tile([P, P], F32, name="own_t", tag="z_row3")
         nc.tensor.transpose(out=own_t[:], in_=own[:], identity=identity[:])
         overall = const.tile([P, 1], F32, name="overall")
         nc.vector.tensor_reduce(out=overall[:], in_=own_t[:], axis=AXIS_X, op=ALU.max)
-        overall_t = psum.tile([P, P], F32, name="overall_t", tag="sum1")
+        bank3 = open_row(3, "sum1")
+        spread(bank3, VECTOR_DIMS + 2, range(PACK))
+        overall_t = psum.tile([P, P], F32, name="overall_t", tag="z_row0")
         nc.tensor.transpose(
             out=overall_t[:], in_=overall[:, 0:1].to_broadcast([P, P]), identity=identity[:]
         )
+        spread(bank3, VECTOR_DIMS + 2, range(PACK, SLABS))
+        keep_row(3, bank3)
+        bank1 = open_row(1, "acc0")
+        spread(bank1, VECTOR_DIMS, range(SLABS))
+        keep_row(1, bank1)
+        bank4 = open_row(4, "acc1")
+        spread(bank4, VECTOR_DIMS + 3, range(SLABS))
+        keep_row(4, bank4)
+
         bounds = const.tile([P, 2 * DIMS], F32, name="bounds")
         nc.vector.tensor_copy(out=bounds[:], in_=overall_t[:, 0 : 2 * DIMS])
         inv_span = const.tile([P, DIMS], F32, name="inv_span")
@@ -118,15 +143,20 @@ def tile_tmgp_sg_kernel(tc, x, design_points, chol_inv_words, chol_inv_scales, o
             out=xs[:], in0=xs[:], in1=inv_span[:].unsqueeze(1).to_broadcast(every_tile)
         )
         neg_half = const.tile(every_tile, F32, name="neg_half")
-        nc.vector.tensor_scalar_mul(out=neg_half[:], in0=xs[:], scalar1=-0.5)
+        nc.scalar.activation(out=neg_half[:], in_=xs[:], func=ACT.Copy, scale=-0.5)
+        xs_sum = const.tile([P, N_TILES], F32, name="xs_sum")
+        nc.vector.tensor_reduce(out=xs_sum[:], in_=xs[:, :, 0:MAX_DIMS], axis=AXIS_X, op=ALU.add)
         shift = const.tile([P, N_TILES], F32, name="shift")
-        nc.vector.tensor_reduce(
-            out=shift[:], in_=neg_half[:, :, 0:MAX_DIMS], axis=AXIS_X, op=ALU.add
-        )
+        nc.vector.tensor_scalar_mul(out=shift[:], in0=xs_sum[:], scalar1=-0.5)
+
+        z_rows = {}
+        for k in TERM_ORDER:
+            d = k - 1
+            z_rows[d] = psum.tile([P, M_PTS], BF16, name="z_row%d" % d)
+            spread(z_rows[d], d, range(SLABS))
 
         out_tiles = out.rearrange("(p i) c -> i p c", i=N_TILES)
-        rows = const.tile([P, TERMS, M_PTS], F32, name="rows")
-        shared_row = const.tile([P, PASSES, P], F32, name="shared_row")
+        shared_row = const.tile([P, PASSES, P], BF16, name="shared_row")
 
         terms = {}
         half_l1 = {}
@@ -137,30 +167,16 @@ def tile_tmgp_sg_kernel(tc, x, design_points, chol_inv_words, chol_inv_scales, o
         acc = {}
         result = {}
 
-        def build_row(k, bank_kind):
-            column = VECTOR_DIMS + k - 1
-            for g in range(PASSES):
-                spread = psum.tile([P, PACK, P], F32, name="spread", tag=bank_kind % g)
-                for t in range(PACK):
-                    nc.tensor.transpose(
-                        out=spread[:, t, :],
-                        in_=z32[:, g * PACK + t, column : column + 1].to_broadcast([P, P]),
-                        identity=identity[:],
-                    )
-                half_row = rows[:, k - 1, g * K_PASS : (g + 1) * K_PASS]
-                if g == 0:
-                    nc.vector.tensor_copy(out=half_row, in_=spread[:].rearrange("p t q -> p (t q)"))
-                else:
-                    nc.scalar.copy(out=half_row, in_=spread[:].rearrange("p t q -> p (t q)"))
-
-        def start_term(i, k):
+        def start_term(i, k, halves=BOTH):
             d = VECTOR_DIMS + k - 1
-            term = work.tile([P, M_PTS], F32, name="term%d" % k)
-            terms[i, k] = term
+            if (i, k) not in terms:
+                terms[i, k] = work.tile([P, M_PTS], F32, name="term%d" % k)
+            term = terms[i, k]
             if k == 1:
+                columns = slice(halves[0] * K_PASS, (halves[-1] + 1) * K_PASS)
                 nc.vector.tensor_scalar(
-                    out=term[:],
-                    in0=rows[:, k - 1, :],
+                    out=term[:, columns],
+                    in0=rows[:, k - 1, columns],
                     scalar1=xs[:, i, d : d + 1],
                     scalar2=shift[:, i : i + 1],
                     op0=ALU.max,
@@ -184,13 +200,14 @@ def tile_tmgp_sg_kernel(tc, x, design_points, chol_inv_words, chol_inv_scales, o
                     bias=neg_half[:, i, d : d + 1],
                 )
 
-        def extend_term(i, k):
+        def extend_term(i, k, halves=BOTH):
             d = k - 1
             width = VECTOR_SLABS * P if d == SHARED else K_PASS
-            term = terms[i, k][:].rearrange("p (g c) -> p g c", g=PASSES)[:, :, 0:width]
+            some = slice(halves[0], halves[-1] + 1)
+            term = terms[i, k][:].rearrange("p (g c) -> p g c", g=PASSES)[:, some, 0:width]
             nc.vector.scalar_tensor_tensor(
                 out=term,
-                in0=z_rows[d][:].rearrange("p (g c) -> p g c", g=PASSES)[:, :, 0:width],
+                in0=z_rows[d][:].rearrange("p (g c) -> p g c", g=PASSES)[:, some, 0:width],
                 scalar=xs[:, i, d : d + 1],
                 in1=term,
                 op0=ALU.max,
@@ -245,68 +262,81 @@ def tile_tmgp_sg_kernel(tc, x, design_points, chol_inv_words, chol_inv_scales, o
                     bias=z_sum[:, slab : slab + 1],
                 )
 
-        def interleave(i):
-            k_star[i] = single.tile([P, PASSES, P, PACK], BF16, name="k_star", align_bytes=64)
+        def interleave(i, halves=BOTH, tag="k_star"):
+            if i not in k_star:
+                k_star[i] = single.tile(
+                    [P, PASSES, P, PACK], BF16, name="k_star", tag=tag, align_bytes=64
+                )
+            some = slice(halves[0], halves[-1] + 1)
             nc.gpsimd.tensor_scalar(
-                out=k_star[i][:],
-                in0=planar[i][:].rearrange("p g t n -> p g n t"),
+                out=k_star[i][:, some, :, :],
+                in0=planar[i][:, some, :, :].rearrange("p g t n -> p g n t"),
                 scalar1=1.0,
                 scalar2=0.0,
                 op0=ALU.mult,
                 op1=ALU.add,
             )
 
-        def quantise(i):
-            k_words[i] = work.tile([P, PASSES * P], U32, name="k_words", align_bytes=64)
-            k_scales[i] = work.tile([P, PASSES * P], U8, name="k_scales", align_bytes=64)
+        def quantise(i, halves=BOTH):
+            if i not in k_words:
+                k_words[i] = work.tile([P, PASSES * P], U32, name="k_words", align_bytes=64)
+                k_scales[i] = work.tile([P, PASSES * P], U8, name="k_scales", align_bytes=64)
+            some = slice(halves[0], halves[-1] + 1)
+            columns = slice(halves[0] * P, (halves[-1] + 1) * P)
             nc.vector.quantize_mx(
-                out=k_words[i][:].bitcast(FP8X4),
-                scales=k_scales[i][:],
-                in_=k_star[i][:].rearrange("p g n t -> p (g n t)"),
+                out=k_words[i][:, columns].bitcast(FP8X4),
+                scales=k_scales[i][:, columns],
+                in_=k_star[i][:, some, :, :].rearrange("p g n t -> p (g n t)"),
+            )
+
+        def open_product(i, h, tag):
+            acc[i, h] = psum.tile([P, BANK], F32, name="acc", tag=tag)
+
+        def multiply_pass(i, h, g):
+            nc.tensor.matmul_mx(
+                out=acc[i, h][:],
+                lhsT=k_words[i][:, g * P : (g + 1) * P].bitcast(FP8X4),
+                lhsT_scale=k_scales[i][:, g * P : (g + 1) * P],
+                rhs=w_words[:, g, h * BANK : (h + 1) * BANK].bitcast(FP8X4),
+                rhs_scale=w_scales[:, g, h * BANK : (h + 1) * BANK],
+                start=(g == 0),
+                stop=(g == PASSES - 1),
             )
 
         def multiply(i, h):
-            acc[i, h] = psum.tile([P, BANK], F32, name="acc", tag="acc%d" % h)
+            open_product(i, h, "acc%d" % h)
             for g in range(PASSES):
-                nc.tensor.matmul_mx(
-                    out=acc[i, h][:],
-                    lhsT=k_words[i][:, g * P : (g + 1) * P].bitcast(FP8X4),
-                    lhsT_scale=k_scales[i][:, g * P : (g + 1) * P],
-                    rhs=w_words[:, g, h * BANK : (h + 1) * BANK].bitcast(FP8X4),
-                    rhs_scale=w_scales[:, g, h * BANK : (h + 1) * BANK],
-                    start=(g == 0),
-                    stop=(g == PASSES - 1),
-                )
+                multiply_pass(i, h, g)
 
-        def copy_out(i, h):
+        def copy_out(i, h, on_vector=False):
             if h == 0:
                 result[i] = work.tile([P, N_COLS], F32, name="result")
-            nc.scalar.copy(out=result[i][:, h * BANK : (h + 1) * BANK], in_=acc[i, h][:])
-            if h == HALVES - 1:
-                nc.sync.dma_start(out=out_tiles[i], in_=result[i][:])
+            columns = slice(h * BANK, (h + 1) * BANK)
+            if on_vector:
+                nc.vector.tensor_copy(out=result[i][:, columns], in_=acc[i, h][:])
+            else:
+                nc.scalar.copy(out=result[i][:, columns], in_=acc[i, h][:])
+
+        def store(i, columns=slice(0, N_COLS)):
+            nc.sync.dma_start(out=out_tiles[i][:, columns], in_=result[i][:, columns])
 
         def live(i):
             return 0 <= i < N_TILES
 
-        spread_shared = psum.tile([P, PASSES, P], F32, name="spread_shared", tag="acc1")
-        for g in range(PASSES):
-            nc.tensor.transpose(
-                out=spread_shared[:, g, :],
-                in_=z32[:, g * PACK + PACK - 1, SHARED : SHARED + 1].to_broadcast([P, P]),
-                identity=identity[:],
-            )
-        nc.scalar.copy(out=shared_row[:], in_=spread_shared[:])
+        start_term(0, 2)
+        start_term(0, 3)
+        start_term(0, 1)
+        start_term(0, 4)
+        nc.scalar.copy(
+            out=shared_row[:],
+            in_=z_rows[SHARED][:].rearrange("p (g c) -> p g c", g=PASSES)[:, :, VECTOR_SLABS * P : K_PASS],
+        )
         start_shared(0)
-        previous = None
-        for place, k in enumerate(TERM_ORDER):
-            build_row(k, "sum%d" if place % 2 == 0 else "acc%d")
-            start_term(0, k)
-            if previous is not None:
-                extend_term(0, previous)
-            previous = k
-        extend_term(0, previous)
+        for k in TERM_ORDER:
+            extend_term(0, k)
 
-        for step in range(N_TILES + 4):
+        last = N_TILES - 1
+        for step in range(N_TILES):
             if live(step - 3):
                 quantise(step - 3)
             if live(step - 2):
@@ -317,6 +347,7 @@ def tile_tmgp_sg_kernel(tc, x, design_points, chol_inv_words, chol_inv_scales, o
             for half in range(2):
                 if half == 0 and live(step - 4):
                     copy_out(step - 4, 1)
+                    store(step - 4)
                 if half == 1 and live(step - 3):
                     copy_out(step - 3, 0)
                 if live(step + 1):
@@ -327,7 +358,39 @@ def tile_tmgp_sg_kernel(tc, x, design_points, chol_inv_words, chol_inv_scales, o
                     multiply(step - 3, half)
                 if live(step - 1):
                     exponential(step - 1, half)
-            if live(step) and step > 0:
+            if 0 < step < last:
                 start_term(step, 1)
                 for k in TERM_ORDER:
                     extend_term(step, k)
+        for g in range(PASSES):
+            start_term(last, 1, (g,))
+            for k in TERM_ORDER:
+                extend_term(last, k, (g,))
+
+        quantise(last - 2)
+        interleave(last - 1)
+        copy_out(last - 3, 1)
+        store(last - 3)
+        for g in range(PASSES):
+            sum_half(last, g)
+            exponential(last, g)
+            interleave(last, (g,), "k_star_last")
+        quantise(last - 1)
+        for g in range(PASSES):
+            quantise(last, (g,))
+        for i, tags in ((last - 2, ("acc0", "acc1")), (last - 1, ("z_row0", "z_row1"))):
+            for h in range(HALVES):
+                open_product(i, h, tags[h])
+                for g in range(PASSES):
+                    multiply_pass(i, h, g)
+            for h in range(HALVES):
+                copy_out(i, h, on_vector=(h == 1))
+            store(i)
+        for h in range(HALVES):
+            open_product(last, h, "z_row%d" % (2 + h))
+        for g in range(PASSES):
+            for h in range(HALVES):
+                multiply_pass(last, h, g)
+        for h in range(HALVES):
+            copy_out(last, h, on_vector=(h == 1))
+            store(last, slice(h * BANK, (h + 1) * BANK))

@@ -32,6 +32,7 @@ TERM_ORDER = (2, 3, 4, 1)
 BOTH = (0, 1)
 SHARED = VECTOR_DIMS - 1
 VECTOR_SLABS = PACK - 1
+EARLY = ((1, 0), (0,), (0,))
 LARGEST = 3.4028234663852886e38
 
 FLOPS = 2 * N_ROWS * M_PTS * N_COLS
@@ -101,10 +102,15 @@ def tile_tmgp_sg_kernel(tc, x, design_points, chol_inv_words, chol_inv_scales, o
         lowest = const.tile([P, DIMS], F32, name="lowest")
         nc.vector.tensor_reduce(out=lowest[:], in_=by_dim, axis=AXIS_X, op=ALU.min)
         nc.vector.tensor_scalar_mul(out=own[:, DIMS : 2 * DIMS], in0=lowest[:], scalar1=-1.0)
-        x32 = const.tile([P, N_TILES, DIMS], F32, name="x32")
-        nc.vector.tensor_copy(out=x32[:], in_=x_bf[:])
-        z_sum = const.tile([P, SLABS], F32, name="z_sum")
-        nc.vector.tensor_reduce(out=z_sum[:], in_=z_bf[:, :, 0:MAX_DIMS], axis=AXIS_X, op=ALU.add)
+        def max_end(j):
+            return MAX_DIMS + 1 if j else MAX_DIMS
+
+        z_sum = {}
+        for j in range(3):
+            z_sum[j] = const.tile([P, SLABS], F32, name="z_sum%d" % j)
+            nc.vector.tensor_reduce(
+                out=z_sum[j][:], in_=z_bf[:, :, j : max_end(j)], axis=AXIS_X, op=ALU.add
+            )
 
         bank2 = open_row(2, "sum0")
         spread(bank2, VECTOR_DIMS + 1, range(SLABS))
@@ -128,36 +134,51 @@ def tile_tmgp_sg_kernel(tc, x, design_points, chol_inv_words, chol_inv_scales, o
         spread(bank4, VECTOR_DIMS + 3, range(SLABS))
         keep_row(4, bank4)
 
-        bounds = const.tile([P, 2 * DIMS], F32, name="bounds")
-        nc.vector.tensor_copy(out=bounds[:], in_=overall_t[:, 0 : 2 * DIMS])
-        inv_span = const.tile([P, DIMS], F32, name="inv_span")
-        nc.vector.tensor_add(out=inv_span[:], in0=bounds[:, 0:DIMS], in1=bounds[:, DIMS : 2 * DIMS])
-        nc.vector.reciprocal(out=inv_span[:], in_=inv_span[:])
-
-        every_tile = [P, N_TILES, DIMS]
-        xs = const.tile(every_tile, F32, name="xs")
-        nc.vector.tensor_add(
-            out=xs[:], in0=x32[:], in1=bounds[:, DIMS : 2 * DIMS].unsqueeze(1).to_broadcast(every_tile)
-        )
-        nc.vector.tensor_mul(
-            out=xs[:], in0=xs[:], in1=inv_span[:].unsqueeze(1).to_broadcast(every_tile)
-        )
-        neg_half = const.tile(every_tile, F32, name="neg_half")
-        nc.scalar.activation(out=neg_half[:], in_=xs[:], func=ACT.Copy, scale=-0.5)
-        xs_sum = const.tile([P, N_TILES], F32, name="xs_sum")
-        nc.vector.tensor_reduce(out=xs_sum[:], in_=xs[:, :, 0:MAX_DIMS], axis=AXIS_X, op=ALU.add)
-        shift = const.tile([P, N_TILES], F32, name="shift")
-        nc.vector.tensor_scalar_mul(out=shift[:], in0=xs_sum[:], scalar1=-0.5)
-
         z_rows = {}
-        for k in TERM_ORDER:
-            d = k - 1
+
+        def spread_for_good(d):
             z_rows[d] = psum.tile([P, M_PTS], BF16, name="z_row%d" % d)
             spread(z_rows[d], d, range(SLABS))
 
-        out_tiles = out.rearrange("(p i) c -> i p c", i=N_TILES)
+        for d in (3, 2, 1):
+            spread_for_good(d)
+
         shared_row = const.tile([P, PASSES, P], BF16, name="shared_row")
 
+        every_tile = [P, N_TILES, DIMS]
+        inv_span = const.tile([P, DIMS], F32, name="inv_span")
+        nc.vector.tensor_copy(out=inv_span[:], in_=overall_t[:, 0:DIMS])
+        xs = const.tile(every_tile, F32, name="xs")
+        nc.vector.tensor_add(
+            out=xs[:],
+            in0=x_bf[:],
+            in1=overall_t[:, DIMS : 2 * DIMS].unsqueeze(1).to_broadcast(every_tile),
+        )
+        nc.vector.tensor_add(out=inv_span[:], in0=inv_span[:], in1=overall_t[:, DIMS : 2 * DIMS])
+        nc.vector.reciprocal(out=inv_span[:], in_=inv_span[:])
+        nc.vector.tensor_mul(
+            out=xs[:], in0=xs[:], in1=inv_span[:].unsqueeze(1).to_broadcast(every_tile)
+        )
+        early = len(EARLY)
+        nc.scalar.copy(
+            out=shared_row[:],
+            in_=z_rows[SHARED][:].rearrange("p (g c) -> p g c", g=PASSES)[:, :, VECTOR_SLABS * P : K_PASS],
+        )
+        neg_half = const.tile(every_tile, F32, name="neg_half")
+        nc.scalar.activation(out=neg_half[:, 0:early, :], in_=xs[:, 0:early, :], func=ACT.Copy, scale=-0.5)
+        xs_sum = const.tile([P, N_TILES], F32, name="xs_sum")
+        shift = const.tile([P, N_TILES], F32, name="shift")
+        for i in range(early):
+            nc.vector.tensor_reduce(
+                out=xs_sum[:, i : i + 1],
+                in_=xs[:, i, len(EARLY[i]) : max_end(len(EARLY[i]))],
+                axis=AXIS_X,
+                op=ALU.add,
+            )
+        nc.vector.tensor_scalar_mul(out=shift[:, 0:early], in0=xs_sum[:, 0:early], scalar1=-0.5)
+        spread_for_good(0)
+
+        out_tiles = out.rearrange("(p i) c -> i p c", i=N_TILES)
         terms = {}
         half_l1 = {}
         planar = {}
@@ -182,7 +203,7 @@ def tile_tmgp_sg_kernel(tc, x, design_points, chol_inv_words, chol_inv_scales, o
                     op0=ALU.max,
                     op1=ALU.add,
                 )
-            elif k == 2:
+            elif k == 2 or (k == 3 and i < early):
                 nc.gpsimd.tensor_scalar(
                     out=term[:],
                     in0=rows[:, k - 1, :],
@@ -200,8 +221,17 @@ def tile_tmgp_sg_kernel(tc, x, design_points, chol_inv_words, chol_inv_scales, o
                     bias=neg_half[:, i, d : d + 1],
                 )
 
-        def extend_term(i, k, halves=BOTH):
-            d = k - 1
+        def start_early(i, d):
+            terms[i, "early", d] = work.tile([P, M_PTS], F32, name="early%d" % d)
+            nc.scalar.activation(
+                out=terms[i, "early", d][:],
+                in_=z_rows[d][:],
+                func=ACT.Abs,
+                scale=0.5,
+                bias=neg_half[:, i, d : d + 1],
+            )
+
+        def extend_term(i, k, d, halves=BOTH):
             width = VECTOR_SLABS * P if d == SHARED else K_PASS
             some = slice(halves[0], halves[-1] + 1)
             term = terms[i, k][:].rearrange("p (g c) -> p g c", g=PASSES)[:, some, 0:width]
@@ -229,6 +259,8 @@ def tile_tmgp_sg_kernel(tc, x, design_points, chol_inv_words, chol_inv_scales, o
             bank = psum.tile([P, PACK, P], F32, name="half_l1", tag="sum%d" % g)
             half_l1[i, g] = bank
             sources = [terms[i, k][:] for k in TERM_ORDER]
+            if i < early:
+                sources += [terms[i, "early", d][:] for d in EARLY[i]]
             for place, source in enumerate(sources):
                 for t in range(PACK):
                     slab = g * PACK + t
@@ -259,22 +291,25 @@ def tile_tmgp_sg_kernel(tc, x, design_points, chol_inv_words, chol_inv_scales, o
                     in_=half_l1[i, g][:, t, :],
                     func=ACT.Exp,
                     scale=-2.0,
-                    bias=z_sum[:, slab : slab + 1],
+                    bias=z_sum[len(EARLY[i]) if i < early else 0][:, slab : slab + 1],
                 )
 
-        def interleave(i, halves=BOTH, tag="k_star"):
-            if i not in k_star:
-                k_star[i] = single.tile(
-                    [P, PASSES, P, PACK], BF16, name="k_star", tag=tag, align_bytes=64
-                )
-            some = slice(halves[0], halves[-1] + 1)
+        def interleave(i):
+            k_star[i] = single.tile([P, PASSES, P, PACK], BF16, name="k_star", align_bytes=64)
             nc.gpsimd.tensor_scalar(
-                out=k_star[i][:, some, :, :],
-                in0=planar[i][:, some, :, :].rearrange("p g t n -> p g n t"),
+                out=k_star[i][:],
+                in0=planar[i][:].rearrange("p g t n -> p g n t"),
                 scalar1=1.0,
                 scalar2=0.0,
                 op0=ALU.mult,
                 op1=ALU.add,
+            )
+
+        def interleave_last(g):
+            if g == 0:
+                k_star[last] = single.tile([P, PASSES, P, PACK], BF16, name="k_star_last", align_bytes=64)
+            nc.vector.tensor_copy(
+                out=k_star[last][:, g, :, :], in_=planar[last][:, g, :, :].rearrange("p t n -> p n t")
             )
 
         def quantise(i, halves=BOTH):
@@ -325,15 +360,22 @@ def tile_tmgp_sg_kernel(tc, x, design_points, chol_inv_words, chol_inv_scales, o
 
         start_term(0, 2)
         start_term(0, 3)
+        start_shared(0)
         start_term(0, 1)
         start_term(0, 4)
-        nc.scalar.copy(
-            out=shared_row[:],
-            in_=z_rows[SHARED][:].rearrange("p (g c) -> p g c", g=PASSES)[:, :, VECTOR_SLABS * P : K_PASS],
+        for d in EARLY[0]:
+            start_early(0, d)
+        nc.scalar.activation(
+            out=neg_half[:, early:N_TILES, :], in_=xs[:, early:N_TILES, :], func=ACT.Copy, scale=-0.5
         )
-        start_shared(0)
-        for k in TERM_ORDER:
-            extend_term(0, k)
+        nc.vector.tensor_reduce(
+            out=xs_sum[:, early:N_TILES], in_=xs[:, early:N_TILES, 0:MAX_DIMS], axis=AXIS_X, op=ALU.add
+        )
+        nc.vector.tensor_scalar_mul(
+            out=shift[:, early:N_TILES], in0=xs_sum[:, early:N_TILES], scalar1=-0.5
+        )
+        extend_term(0, 1, 3)
+        extend_term(0, 2, 2)
 
         last = N_TILES - 1
         for step in range(N_TILES):
@@ -343,6 +385,8 @@ def tile_tmgp_sg_kernel(tc, x, design_points, chol_inv_words, chol_inv_scales, o
                 interleave(step - 2)
             if live(step + 1):
                 start_term(step + 1, 2)
+                if step + 1 < early:
+                    start_term(step + 1, 3)
                 start_shared(step + 1)
             for half in range(2):
                 if half == 0 and live(step - 4):
@@ -350,7 +394,9 @@ def tile_tmgp_sg_kernel(tc, x, design_points, chol_inv_words, chol_inv_scales, o
                     store(step - 4)
                 if half == 1 and live(step - 3):
                     copy_out(step - 3, 0)
-                if live(step + 1):
+                if half == 0 and step + 1 < early:
+                    start_early(step + 1, 0)
+                elif live(step + 1):
                     start_term(step + 1, 3 + half)
                 if live(step - 1):
                     sum_half(step - 1, half)
@@ -360,34 +406,41 @@ def tile_tmgp_sg_kernel(tc, x, design_points, chol_inv_words, chol_inv_scales, o
                     exponential(step - 1, half)
             if 0 < step < last:
                 start_term(step, 1)
-                for k in TERM_ORDER:
-                    extend_term(step, k)
-        for g in range(PASSES):
-            start_term(last, 1, (g,))
-            for k in TERM_ORDER:
-                extend_term(last, k, (g,))
-
-        quantise(last - 2)
-        interleave(last - 1)
+                if step < early:
+                    for k in (1, 2, 3):
+                        extend_term(step, k, k)
+                else:
+                    for k in TERM_ORDER:
+                        extend_term(step, k, k - 1)
         copy_out(last - 3, 1)
         store(last - 3)
         for g in range(PASSES):
+            start_term(last, 1, (g,))
+            for k in TERM_ORDER:
+                extend_term(last, k, k - 1, (g,))
             sum_half(last, g)
             exponential(last, g)
-            interleave(last, (g,), "k_star_last")
+            if g == 0:
+                quantise(last - 2)
+                interleave(last - 1)
+        for h in range(HALVES):
+            multiply(last - 2, h)
         quantise(last - 1)
         for g in range(PASSES):
+            interleave_last(g)
             quantise(last, (g,))
-        for i, tags in ((last - 2, ("acc0", "acc1")), (last - 1, ("z_row0", "z_row1"))):
-            for h in range(HALVES):
-                open_product(i, h, tags[h])
-                for g in range(PASSES):
-                    multiply_pass(i, h, g)
-            for h in range(HALVES):
-                copy_out(i, h, on_vector=(h == 1))
-            store(i)
         for h in range(HALVES):
+            copy_out(last - 2, h, on_vector=(h == 1))
+        store(last - 2)
+        for h in range(HALVES):
+            open_product(last - 1, h, "z_row%d" % h)
             open_product(last, h, "z_row%d" % (2 + h))
+        for h in range(HALVES):
+            for g in range(PASSES):
+                multiply_pass(last - 1, h, g)
+        for h in range(HALVES):
+            copy_out(last - 1, h, on_vector=(h == 1))
+        store(last - 1)
         for g in range(PASSES):
             for h in range(HALVES):
                 multiply_pass(last, h, g)

@@ -52,6 +52,18 @@ def tile_tmgp_sg_kernel(tc, x, design_points, chol_inv_words, chol_inv_scales, o
         identity_bf = const.tile([P, P], BF16, name="identity_bf")
         make_identity(nc, identity_bf[:])
 
+        idle_rhs = const.tile([P, BANK], BF16, name="idle_rhs")
+        nc.gpsimd.memset(idle_rhs[:], 0.0)
+
+        def keep_warm(bank, count=2):
+            for repeat in range(count):
+                nc.tensor.matmul(
+                    out=bank[:], lhsT=identity_bf[:], rhs=idle_rhs[:], start=True, stop=True
+                )
+
+        idle_bank = psum.tile([P, BANK], F32, name="idle_bank", tag="z_row1")
+        keep_warm(idle_bank, 4)
+
         zero = const.tile([P, 1], F32, name="zero")
         nc.vector.memset(zero[:], 0.0)
         warm = const.tile([P, 1], F32, name="warm")
@@ -114,6 +126,7 @@ def tile_tmgp_sg_kernel(tc, x, design_points, chol_inv_words, chol_inv_scales, o
 
         bank2 = open_row(2, "sum0")
         spread(bank2, VECTOR_DIMS + 1, range(SLABS))
+        keep_warm(idle_bank)
         keep_row(2, bank2)
         own_t = psum.tile([P, P], F32, name="own_t", tag="z_row3")
         nc.tensor.transpose(out=own_t[:], in_=own[:], identity=identity[:])
@@ -126,9 +139,11 @@ def tile_tmgp_sg_kernel(tc, x, design_points, chol_inv_words, chol_inv_scales, o
             out=overall_t[:], in_=overall[:, 0:1].to_broadcast([P, P]), identity=identity[:]
         )
         spread(bank3, VECTOR_DIMS + 2, range(PACK, SLABS))
+        keep_warm(idle_bank)
         keep_row(3, bank3)
         bank1 = open_row(1, "acc0")
         spread(bank1, VECTOR_DIMS, range(SLABS))
+        keep_warm(idle_bank)
         keep_row(1, bank1)
         bank4 = open_row(4, "acc1")
         spread(bank4, VECTOR_DIMS + 3, range(SLABS))
@@ -140,8 +155,12 @@ def tile_tmgp_sg_kernel(tc, x, design_points, chol_inv_words, chol_inv_scales, o
             z_rows[d] = psum.tile([P, M_PTS], BF16, name="z_row%d" % d)
             spread(z_rows[d], d, range(SLABS))
 
-        for d in (3, 2, 1):
-            spread_for_good(d)
+        spread_for_good(3)
+        keep_warm(idle_bank)
+        spread_for_good(2)
+        spread_for_good(1)
+        idle_bank = psum.tile([P, BANK], F32, name="idle_bank", tag="acc0")
+        keep_warm(idle_bank)
 
         shared_row = const.tile([P, PASSES, P], BF16, name="shared_row")
 
@@ -258,10 +277,14 @@ def tile_tmgp_sg_kernel(tc, x, design_points, chol_inv_words, chol_inv_scales, o
         def sum_half(i, g):
             bank = psum.tile([P, PACK, P], F32, name="half_l1", tag="sum%d" % g)
             half_l1[i, g] = bank
-            sources = [terms[i, k][:] for k in TERM_ORDER]
             if i < early:
-                sources += [terms[i, "early", d][:] for d in EARLY[i]]
+                sources = [terms[i, 4][:]] + [terms[i, "early", d][:] for d in EARLY[i]]
+                sources += [terms[i, k][:] for k in ((3, 1, 2) if i == 0 else (1, 2, 3))]
+            else:
+                sources = [terms[i, k][:] for k in TERM_ORDER]
             for place, source in enumerate(sources):
+                if i + 1 < early and place % 3 == 2:
+                    keep_warm(idle_bank)
                 for t in range(PACK):
                     slab = g * PACK + t
                     nc.tensor.matmul(

@@ -31,7 +31,8 @@ TERMS = DIMS - VECTOR_DIMS
 TERM_ORDER = (2, 3, 4, 1)
 BOTH = (0, 1)
 SHARED = VECTOR_DIMS - 1
-VECTOR_SLABS = PACK - 1
+VECTOR_FROM, VECTOR_TO = 1, 6
+SHORT_SLABS = (0, 6, 7)
 EARLY = ((1, 0), (0,), (0,))
 LARGEST = 3.4028234663852886e38
 
@@ -162,7 +163,7 @@ def tile_tmgp_sg_kernel(tc, x, design_points, chol_inv_words, chol_inv_scales, o
         idle_bank = psum.tile([P, BANK], F32, name="idle_bank", tag="acc0")
         keep_warm(idle_bank)
 
-        shared_row = const.tile([P, PASSES, P], BF16, name="shared_row")
+        shared_row = const.tile([P, len(SHORT_SLABS), P], BF16, name="shared_row")
 
         every_tile = [P, N_TILES, DIMS]
         inv_span = const.tile([P, DIMS], F32, name="inv_span")
@@ -179,9 +180,10 @@ def tile_tmgp_sg_kernel(tc, x, design_points, chol_inv_words, chol_inv_scales, o
             out=xs[:], in0=xs[:], in1=inv_span[:].unsqueeze(1).to_broadcast(every_tile)
         )
         early = len(EARLY)
+        nc.scalar.copy(out=shared_row[:, 0, :], in_=z_rows[SHARED][:, 0:P])
         nc.scalar.copy(
-            out=shared_row[:],
-            in_=z_rows[SHARED][:].rearrange("p (g c) -> p g c", g=PASSES)[:, :, VECTOR_SLABS * P : K_PASS],
+            out=shared_row[:, 1:3, :].rearrange("p s c -> p (s c)"),
+            in_=z_rows[SHARED][:, VECTOR_TO * P : M_PTS],
         )
         neg_half = const.tile(every_tile, F32, name="neg_half")
         nc.scalar.activation(out=neg_half[:, 0:early, :], in_=xs[:, 0:early, :], func=ACT.Copy, scale=-0.5)
@@ -251,12 +253,13 @@ def tile_tmgp_sg_kernel(tc, x, design_points, chol_inv_words, chol_inv_scales, o
             )
 
         def extend_term(i, k, d, halves=BOTH):
-            width = VECTOR_SLABS * P if d == SHARED else K_PASS
-            some = slice(halves[0], halves[-1] + 1)
-            term = terms[i, k][:].rearrange("p (g c) -> p g c", g=PASSES)[:, some, 0:width]
+            start, end = halves[0] * K_PASS, (halves[-1] + 1) * K_PASS
+            if d == SHARED:
+                start, end = max(start, VECTOR_FROM * P), min(end, VECTOR_TO * P)
+            term = terms[i, k][:, start:end]
             nc.vector.scalar_tensor_tensor(
                 out=term,
-                in0=z_rows[d][:].rearrange("p (g c) -> p g c", g=PASSES)[:, some, 0:width],
+                in0=z_rows[d][:, start:end],
                 scalar=xs[:, i, d : d + 1],
                 in1=term,
                 op0=ALU.max,
@@ -264,7 +267,7 @@ def tile_tmgp_sg_kernel(tc, x, design_points, chol_inv_words, chol_inv_scales, o
             )
 
         def start_shared(i):
-            terms[i, 0] = work.tile([P, PASSES, P], F32, name="term0")
+            terms[i, 0] = work.tile([P, len(SHORT_SLABS), P], F32, name="term0")
             nc.gpsimd.tensor_scalar(
                 out=terms[i, 0][:],
                 in0=shared_row[:],
@@ -295,14 +298,16 @@ def tile_tmgp_sg_kernel(tc, x, design_points, chol_inv_words, chol_inv_scales, o
                         start=(place == 0 and t == 0),
                         stop=False,
                     )
-            nc.tensor.matmul(
-                out=bank[:, PACK - 1, :],
-                lhsT=terms[i, 0][:, g, :],
-                rhs=identity[:],
-                is_transpose=True,
-                start=False,
-                stop=True,
-            )
+            short = [j for j, slab in enumerate(SHORT_SLABS) if slab // PACK == g]
+            for j in short:
+                nc.tensor.matmul(
+                    out=bank[:, SHORT_SLABS[j] % PACK, :],
+                    lhsT=terms[i, 0][:, j, :],
+                    rhs=identity[:],
+                    is_transpose=True,
+                    start=False,
+                    stop=(j == short[-1]),
+                )
 
         def exponential(i, g):
             if g == 0:

@@ -33,6 +33,7 @@ BOTH = (0, 1)
 SHARED = VECTOR_DIMS - 1
 VECTOR_FROM, VECTOR_TO = 1, 6
 SHORT_SLABS = (0, 6, 7)
+UNSHARED = 3
 EARLY = ((1, 0), (0,), (0,))
 LARGEST = 3.4028234663852886e38
 
@@ -48,22 +49,22 @@ def tile_tmgp_sg_kernel(tc, x, design_points, chol_inv_words, chol_inv_scales, o
         psum = stack.enter_context(tc.psum_pool(name="psum", bufs=1))
         stack.enter_context(tc.manual_schedule())
 
-        identity = const.tile([P, P], F32, name="identity")
-        make_identity(nc, identity[:])
-        identity_bf = const.tile([P, P], BF16, name="identity_bf")
-        make_identity(nc, identity_bf[:])
+        zeros = const.tile([P, 2 * P], BF16, name="zeros")
+        nc.vector.memset(zeros[:], 0.0)
 
-        idle_rhs = const.tile([P, BANK], BF16, name="idle_rhs")
-        nc.gpsimd.memset(idle_rhs[:], 0.0)
-
-        def keep_warm(bank, count=2):
-            for repeat in range(count):
+        def keep_warm(bank):
+            for repeat in range(4):
                 nc.tensor.matmul(
-                    out=bank[:], lhsT=identity_bf[:], rhs=idle_rhs[:], start=True, stop=True
+                    out=bank[:], lhsT=zeros[:, 0:P], rhs=zeros[:], start=True, stop=True
                 )
 
-        idle_bank = psum.tile([P, BANK], F32, name="idle_bank", tag="z_row1")
-        keep_warm(idle_bank, 4)
+        idle_bank = psum.tile([P, 2 * P], F32, name="idle_bank", tag="z_row1")
+        keep_warm(idle_bank)
+
+        identity_bf = const.tile([P, P], BF16, name="identity_bf")
+        make_identity(nc, identity_bf[:])
+        identity = const.tile([P, P], F32, name="identity")
+        make_identity(nc, identity[:])
 
         zero = const.tile([P, 1], F32, name="zero")
         nc.vector.memset(zero[:], 0.0)
@@ -108,13 +109,19 @@ def tile_tmgp_sg_kernel(tc, x, design_points, chol_inv_words, chol_inv_scales, o
         def keep_row(k, bank):
             nc.scalar.copy(out=rows[:, k - 1, :], in_=bank[:])
 
-        own = const.tile([P, P], F32, name="own")
-        nc.vector.memset(own[:], 0.0)
-        by_dim = x_bf[:].rearrange("p i d -> p d i")
-        nc.vector.tensor_reduce(out=own[:, 0:DIMS], in_=by_dim, axis=AXIS_X, op=ALU.max)
-        lowest = const.tile([P, DIMS], F32, name="lowest")
-        nc.vector.tensor_reduce(out=lowest[:], in_=by_dim, axis=AXIS_X, op=ALU.min)
-        nc.vector.tensor_scalar_mul(out=own[:, DIMS : 2 * DIMS], in0=lowest[:], scalar1=-1.0)
+        half_tiles = N_TILES // 2
+        x_t = psum.tile([P, 2, P], BF16, name="x_t", tag="z_row3")
+        for h in range(2):
+            nc.tensor.transpose(
+                out=x_t[:, h, :],
+                in_=x_bf[:, h * half_tiles : (h + 1) * half_tiles, :].rearrange("p i d -> p (i d)"),
+                identity=identity_bf[:],
+            )
+        ends = const.tile([P, 2], F32, name="ends")
+        for j, op in enumerate((ALU.min, ALU.max)):
+            nc.vector.tensor_reduce(
+                out=ends[:, j : j + 1], in_=x_t[:].rearrange("p h n -> p (h n)"), axis=AXIS_X, op=op
+            )
         def max_end(j):
             return MAX_DIMS + 1 if j else MAX_DIMS
 
@@ -125,30 +132,22 @@ def tile_tmgp_sg_kernel(tc, x, design_points, chol_inv_words, chol_inv_scales, o
                 out=z_sum[j][:], in_=z_bf[:, :, j : max_end(j)], axis=AXIS_X, op=ALU.add
             )
 
-        bank2 = open_row(2, "sum0")
-        spread(bank2, VECTOR_DIMS + 1, range(SLABS))
+        def bring_row(k, tag):
+            bank = open_row(k, tag)
+            spread(bank, VECTOR_DIMS + k - 1, range(SLABS))
+            keep_row(k, bank)
+
+        bring_row(2, "sum0")
+        ends_t = psum.tile([P, 2, P], F32, name="ends_t", tag="z_row0")
+        for j in range(2):
+            nc.tensor.transpose(
+                out=ends_t[:, j, :], in_=ends[:, j : j + 1].to_broadcast([P, P]), identity=identity[:]
+            )
         keep_warm(idle_bank)
-        keep_row(2, bank2)
-        own_t = psum.tile([P, P], F32, name="own_t", tag="z_row3")
-        nc.tensor.transpose(out=own_t[:], in_=own[:], identity=identity[:])
-        overall = const.tile([P, 1], F32, name="overall")
-        nc.vector.tensor_reduce(out=overall[:], in_=own_t[:], axis=AXIS_X, op=ALU.max)
-        bank3 = open_row(3, "sum1")
-        spread(bank3, VECTOR_DIMS + 2, range(PACK))
-        overall_t = psum.tile([P, P], F32, name="overall_t", tag="z_row0")
-        nc.tensor.transpose(
-            out=overall_t[:], in_=overall[:, 0:1].to_broadcast([P, P]), identity=identity[:]
-        )
-        spread(bank3, VECTOR_DIMS + 2, range(PACK, SLABS))
+        bring_row(1, "sum1")
+        bring_row(4, "acc0")
         keep_warm(idle_bank)
-        keep_row(3, bank3)
-        bank1 = open_row(1, "acc0")
-        spread(bank1, VECTOR_DIMS, range(SLABS))
-        keep_warm(idle_bank)
-        keep_row(1, bank1)
-        bank4 = open_row(4, "acc1")
-        spread(bank4, VECTOR_DIMS + 3, range(SLABS))
-        keep_row(4, bank4)
+        bring_row(3, "acc1")
 
         z_rows = {}
 
@@ -156,35 +155,33 @@ def tile_tmgp_sg_kernel(tc, x, design_points, chol_inv_words, chol_inv_scales, o
             z_rows[d] = psum.tile([P, M_PTS], BF16, name="z_row%d" % d)
             spread(z_rows[d], d, range(SLABS))
 
-        spread_for_good(3)
-        keep_warm(idle_bank)
         spread_for_good(2)
+        keep_warm(idle_bank)
+        spread_for_good(3)
         spread_for_good(1)
-        idle_bank = psum.tile([P, BANK], F32, name="idle_bank", tag="acc0")
+        idle_bank = psum.tile([P, 2 * P], F32, name="idle_bank", tag="acc0")
         keep_warm(idle_bank)
 
         shared_row = const.tile([P, len(SHORT_SLABS), P], BF16, name="shared_row")
 
         every_tile = [P, N_TILES, DIMS]
-        inv_span = const.tile([P, DIMS], F32, name="inv_span")
-        nc.vector.tensor_copy(out=inv_span[:], in_=overall_t[:, 0:DIMS])
+        lowest = const.tile([P, DIMS], F32, name="lowest")
+        highest = const.tile([P, DIMS], F32, name="highest")
+        for j, (bound, op) in enumerate(((lowest, ALU.min), (highest, ALU.max))):
+            nc.vector.tensor_reduce(
+                out=bound[:], in_=ends_t[:, j, :].rearrange("p (i d) -> p d i", d=DIMS), axis=AXIS_X, op=op
+            )
         xs = const.tile(every_tile, F32, name="xs")
-        nc.vector.tensor_add(
-            out=xs[:],
-            in0=x_bf[:],
-            in1=overall_t[:, DIMS : 2 * DIMS].unsqueeze(1).to_broadcast(every_tile),
+        nc.vector.tensor_sub(
+            out=xs[:], in0=x_bf[:], in1=lowest[:].unsqueeze(1).to_broadcast(every_tile)
         )
-        nc.vector.tensor_add(out=inv_span[:], in0=inv_span[:], in1=overall_t[:, DIMS : 2 * DIMS])
+        inv_span = const.tile([P, DIMS], F32, name="inv_span")
+        nc.vector.tensor_sub(out=inv_span[:], in0=highest[:], in1=lowest[:])
         nc.vector.reciprocal(out=inv_span[:], in_=inv_span[:])
         nc.vector.tensor_mul(
             out=xs[:], in0=xs[:], in1=inv_span[:].unsqueeze(1).to_broadcast(every_tile)
         )
         early = len(EARLY)
-        nc.scalar.copy(out=shared_row[:, 0, :], in_=z_rows[SHARED][:, 0:P])
-        nc.scalar.copy(
-            out=shared_row[:, 1:3, :].rearrange("p s c -> p (s c)"),
-            in_=z_rows[SHARED][:, VECTOR_TO * P : M_PTS],
-        )
         neg_half = const.tile(every_tile, F32, name="neg_half")
         nc.scalar.activation(out=neg_half[:, 0:early, :], in_=xs[:, 0:early, :], func=ACT.Copy, scale=-0.5)
         xs_sum = const.tile([P, N_TILES], F32, name="xs_sum")
@@ -252,9 +249,12 @@ def tile_tmgp_sg_kernel(tc, x, design_points, chol_inv_words, chol_inv_scales, o
                 bias=neg_half[:, i, d : d + 1],
             )
 
+        def is_shared(i):
+            return i < N_TILES - UNSHARED
+
         def extend_term(i, k, d, halves=BOTH):
             start, end = halves[0] * K_PASS, (halves[-1] + 1) * K_PASS
-            if d == SHARED:
+            if d == SHARED and is_shared(i):
                 start, end = max(start, VECTOR_FROM * P), min(end, VECTOR_TO * P)
             term = terms[i, k][:, start:end]
             nc.vector.scalar_tensor_tensor(
@@ -285,6 +285,7 @@ def tile_tmgp_sg_kernel(tc, x, design_points, chol_inv_words, chol_inv_scales, o
                 sources += [terms[i, k][:] for k in ((3, 1, 2) if i == 0 else (1, 2, 3))]
             else:
                 sources = [terms[i, k][:] for k in TERM_ORDER]
+            short = [j for j, slab in enumerate(SHORT_SLABS) if is_shared(i) and slab // PACK == g]
             for place, source in enumerate(sources):
                 if i + 1 < early and place % 3 == 2:
                     keep_warm(idle_bank)
@@ -296,9 +297,8 @@ def tile_tmgp_sg_kernel(tc, x, design_points, chol_inv_words, chol_inv_scales, o
                         rhs=identity[:],
                         is_transpose=True,
                         start=(place == 0 and t == 0),
-                        stop=False,
+                        stop=(place == len(sources) - 1 and t == PACK - 1 and not short),
                     )
-            short = [j for j, slab in enumerate(SHORT_SLABS) if slab // PACK == g]
             for j in short:
                 nc.tensor.matmul(
                     out=bank[:, SHORT_SLABS[j] % PACK, :],
@@ -373,7 +373,7 @@ def tile_tmgp_sg_kernel(tc, x, design_points, chol_inv_words, chol_inv_scales, o
 
         def copy_out(i, h, on_vector=False):
             if h == 0:
-                result[i] = work.tile([P, N_COLS], F32, name="result")
+                result[i] = work.tile([P, N_COLS], F32, name="result", bufs=4)
             columns = slice(h * BANK, (h + 1) * BANK)
             if on_vector:
                 nc.vector.tensor_copy(out=result[i][:, columns], in_=acc[i, h][:])
@@ -388,9 +388,14 @@ def tile_tmgp_sg_kernel(tc, x, design_points, chol_inv_words, chol_inv_scales, o
 
         start_term(0, 2)
         start_term(0, 3)
-        start_shared(0)
         start_term(0, 1)
         start_term(0, 4)
+        nc.scalar.copy(out=shared_row[:, 0, :], in_=z_rows[SHARED][:, 0:P])
+        nc.scalar.copy(
+            out=shared_row[:, 1:3, :].rearrange("p s c -> p (s c)"),
+            in_=z_rows[SHARED][:, VECTOR_TO * P : M_PTS],
+        )
+        start_shared(0)
         for d in EARLY[0]:
             start_early(0, d)
         nc.scalar.activation(
@@ -402,8 +407,8 @@ def tile_tmgp_sg_kernel(tc, x, design_points, chol_inv_words, chol_inv_scales, o
         nc.vector.tensor_scalar_mul(
             out=shift[:, early:N_TILES], in0=xs_sum[:, early:N_TILES], scalar1=-0.5
         )
-        extend_term(0, 1, 3)
-        extend_term(0, 2, 2)
+        extend_term(0, 1, 2)
+        extend_term(0, 2, 3)
 
         last = N_TILES - 1
         for step in range(N_TILES):
@@ -415,7 +420,8 @@ def tile_tmgp_sg_kernel(tc, x, design_points, chol_inv_words, chol_inv_scales, o
                 start_term(step + 1, 2)
                 if step + 1 < early:
                     start_term(step + 1, 3)
-                start_shared(step + 1)
+                if is_shared(step + 1):
+                    start_shared(step + 1)
             for half in range(2):
                 if half == 0 and live(step - 4):
                     copy_out(step - 4, 1)

@@ -34,7 +34,7 @@ SHARED = VECTOR_DIMS - 1
 VECTOR_FROM, VECTOR_TO = 1, 6
 SHORT_SLABS = (0, 6, 7)
 UNSHARED = 3
-EARLY = ((1, 0), (0,), (0,))
+EARLY = ((1, 0), (0,))
 LARGEST = 3.4028234663852886e38
 
 FLOPS = 2 * N_ROWS * M_PTS * N_COLS
@@ -287,7 +287,7 @@ def tile_tmgp_sg_kernel(tc, x, design_points, chol_inv_words, chol_inv_scales, o
                 sources = [terms[i, k][:] for k in TERM_ORDER]
             short = [j for j, slab in enumerate(SHORT_SLABS) if is_shared(i) and slab // PACK == g]
             for place, source in enumerate(sources):
-                if i + 1 < early and place % 3 == 2:
+                if i < early and place % 3 == 2:
                     keep_warm(idle_bank)
                 for t in range(PACK):
                     slab = g * PACK + t

from contextlib import ExitStack

import concourse.mybir as mybir
from concourse.masks import make_identity

F32 = mybir.dt.float32
BF16 = mybir.dt.bfloat16
I32 = mybir.dt.int32
U32 = mybir.dt.uint32
U8 = mybir.dt.uint8
FP8X4 = mybir.dt.float8_e4m3fn_x4
ALU = mybir.AluOpType
ACT = mybir.ActivationFunctionType
AXIS_X = mybir.AxisListType.X

P = 128
PACK = 4
K_PASS = P * PACK
N_ROWS = 4096
DIMS = 8
M_PTS = 1024
N_COLS = 1024
PASSES = M_PTS // K_PASS
SLABS = PASSES * PACK
N_TILES = N_ROWS // P
BANK = 512
HALVES = N_COLS // BANK
VECTOR_DIMS = 4
MAX_DIMS = 6
TERMS = DIMS - VECTOR_DIMS
TERM_ORDER = (2, 3, 4, 1)
BOTH = (0, 1)
SHARED = VECTOR_DIMS - 1
VECTOR_FROM, VECTOR_TO = 1, 6
SHORT_SLABS = (0, 6, 7)
UNSHARED = 3
EARLY = ((1, 0), (0,))
LARGEST = 3.4028234663852886e38

FLOPS = 2 * N_ROWS * M_PTS * N_COLS


def tile_tmgp_sg_kernel(tc, x, design_points, chol_inv_words, chol_inv_scales, out):
    nc = tc.nc
    with ExitStack() as stack:
        const = stack.enter_context(tc.tile_pool(name="const", bufs=1))
        work = stack.enter_context(tc.tile_pool(name="work", bufs=3))
        single = stack.enter_context(tc.tile_pool(name="single", bufs=1))
        psum = stack.enter_context(tc.psum_pool(name="psum", bufs=1))
        stack.enter_context(tc.manual_schedule())

        zeros = const.tile([P, 2 * P], BF16, name="zeros")
        nc.vector.memset(zeros[:], 0.0)

        def keep_warm(bank):
            for repeat in range(4):
                nc.tensor.matmul(
                    out=bank[:], lhsT=zeros[:, 0:P], rhs=zeros[:], start=True, stop=True
                )

        idle_bank = psum.tile([P, 2 * P], F32, name="idle_bank", tag="z_row1")
        keep_warm(idle_bank)

        identity_bf = const.tile([P, P], BF16, name="identity_bf")
        make_identity(nc, identity_bf[:])
        identity = const.tile([P, P], F32, name="identity")
        make_identity(nc, identity[:])

        zero = const.tile([P, 1], F32, name="zero")
        nc.vector.memset(zero[:], 0.0)
        warm = const.tile([P, 1], F32, name="warm")
        nc.scalar.activation(out=warm[:], in_=zero[:], func=ACT.Exp)

        x_bf = const.tile([P, N_TILES, DIMS], BF16, name="x_bf")
        nc.sync.dma_start(out=x_bf[:], in_=x.rearrange("(p i) d -> p i d", i=N_TILES))
        z_bf = const.tile([P, SLABS, DIMS], BF16, name="z_bf")
        nc.sync.dma_start(
            out=z_bf[:].rearrange("p (g t) d -> p g (t d)", g=PASSES),
            in_=design_points.rearrange("(g p t) d -> p g (t d)", g=PASSES, t=PACK),
        )
        w_scales = const.tile([P, PASSES, N_COLS], U8, name="w_scales", align_bytes=64)
        nc.vector.memset(w_scales[:].rearrange("p g n -> p (g n)").bitcast(I32), 0)
        for g in range(PASSES):
            for quad in range(4):
                nc.sync.dma_start(
                    out=w_scales[32 * quad : 32 * quad + 4, g, :].bitcast(I32),
                    in_=chol_inv_scales[g, 4 * quad : 4 * quad + 4, :].bitcast(I32),
                )
        w_words = const.tile([P, PASSES, N_COLS], U32, name="w_words", align_bytes=64)
        for g in range(PASSES):
            nc.sync.dma_start(
                out=w_words[:, g, :].bitcast(I32),
                in_=chol_inv_words[g].rearrange("p n t -> p (n t)").bitcast(I32),
            )

        def spread(bank, d, slabs):
            for s in slabs:
                nc.tensor.transpose(
                    out=bank[:, s * P : (s + 1) * P],
                    in_=z_bf[:, s, d : d + 1].to_broadcast([P, P]),
                    identity=identity_bf[:],
                )

        rows = const.tile([P, TERMS, M_PTS], BF16, name="rows")

        def open_row(k, tag):
            return psum.tile([P, M_PTS], BF16, name="row", tag=tag)

        def keep_row(k, bank):
            nc.scalar.copy(out=rows[:, k - 1, :], in_=bank[:])

        half_tiles = N_TILES // 2
        x_t = psum.tile([P, 2, P], BF16, name="x_t", tag="z_row3")
        for h in range(2):
            nc.tensor.transpose(
                out=x_t[:, h, :],
                in_=x_bf[:, h * half_tiles : (h + 1) * half_tiles, :].rearrange("p i d -> p (i d)"),
                identity=identity_bf[:],
            )
        ends = const.tile([P, 2], F32, name="ends")
        for j, op in enumerate((ALU.min, ALU.max)):
            nc.vector.tensor_reduce(
                out=ends[:, j : j + 1], in_=x_t[:].rearrange("p h n -> p (h n)"), axis=AXIS_X, op=op
            )
        def max_end(j):
            return MAX_DIMS + 1 if j else MAX_DIMS

        z_sum = {}
        for j in range(3):
            z_sum[j] = const.tile([P, SLABS], F32, name="z_sum%d" % j)
            nc.vector.tensor_reduce(
                out=z_sum[j][:], in_=z_bf[:, :, j : max_end(j)], axis=AXIS_X, op=ALU.add
            )

        def bring_row(k, tag):
            bank = open_row(k, tag)
            spread(bank, VECTOR_DIMS + k - 1, range(SLABS))
            keep_row(k, bank)

        bring_row(2, "sum0")
        ends_t = psum.tile([P, 2, P], F32, name="ends_t", tag="z_row0")
        for j in range(2):
            nc.tensor.transpose(
                out=ends_t[:, j, :], in_=ends[:, j : j + 1].to_broadcast([P, P]), identity=identity[:]
            )
        keep_warm(idle_bank)
        bring_row(1, "sum1")
        bring_row(4, "acc0")
        keep_warm(idle_bank)
        bring_row(3, "acc1")

        z_rows = {}

        def spread_for_good(d):
            z_rows[d] = psum.tile([P, M_PTS], BF16, name="z_row%d" % d)
            spread(z_rows[d], d, range(SLABS))

        spread_for_good(2)
        keep_warm(idle_bank)
        spread_for_good(3)
        spread_for_good(1)
        idle_bank = psum.tile([P, 2 * P], F32, name="idle_bank", tag="acc0")
        keep_warm(idle_bank)

        shared_row = const.tile([P, len(SHORT_SLABS), P], BF16, name="shared_row")

        every_tile = [P, N_TILES, DIMS]
        lowest = const.tile([P, DIMS], F32, name="lowest")
        highest = const.tile([P, DIMS], F32, name="highest")
        for j, (bound, op) in enumerate(((lowest, ALU.min), (highest, ALU.max))):
            nc.vector.tensor_reduce(
                out=bound[:], in_=ends_t[:, j, :].rearrange("p (i d) -> p d i", d=DIMS), axis=AXIS_X, op=op
            )
        xs = const.tile(every_tile, F32, name="xs")
        nc.vector.tensor_sub(
            out=xs[:], in0=x_bf[:], in1=lowest[:].unsqueeze(1).to_broadcast(every_tile)
        )
        inv_span = const.tile([P, DIMS], F32, name="inv_span")
        nc.vector.tensor_sub(out=inv_span[:], in0=highest[:], in1=lowest[:])
        nc.vector.reciprocal(out=inv_span[:], in_=inv_span[:])
        nc.vector.tensor_mul(
            out=xs[:], in0=xs[:], in1=inv_span[:].unsqueeze(1).to_broadcast(every_tile)
        )
        early = len(EARLY)
        neg_half = const.tile(every_tile, F32, name="neg_half")
        nc.scalar.activation(out=neg_half[:, 0:early, :], in_=xs[:, 0:early, :], func=ACT.Copy, scale=-0.5)
        xs_sum = const.tile([P, N_TILES], F32, name="xs_sum")
        shift = const.tile([P, N_TILES], F32, name="shift")
        for i in range(early):
            nc.vector.tensor_reduce(
                out=xs_sum[:, i : i + 1],
                in_=xs[:, i, len(EARLY[i]) : max_end(len(EARLY[i]))],
                axis=AXIS_X,
                op=ALU.add,
            )
        nc.vector.tensor_scalar_mul(out=shift[:, 0:early], in0=xs_sum[:, 0:early], scalar1=-0.5)
        spread_for_good(0)

        out_tiles = out.rearrange("(p i) c -> i p c", i=N_TILES)
        terms = {}
        half_l1 = {}
        planar = {}
        k_star = {}
        k_words = {}
        k_scales = {}
        acc = {}
        result = {}

        def start_term(i, k, halves=BOTH):
            d = VECTOR_DIMS + k - 1
            if (i, k) not in terms:
                terms[i, k] = work.tile([P, M_PTS], F32, name="term%d" % k)
            term = terms[i, k]
            if k == 1:
                columns = slice(halves[0] * K_PASS, (halves[-1] + 1) * K_PASS)
                nc.vector.tensor_scalar(
                    out=term[:, columns],
                    in0=rows[:, k - 1, columns],
                    scalar1=xs[:, i, d : d + 1],
                    scalar2=shift[:, i : i + 1],
                    op0=ALU.max,
                    op1=ALU.add,
                )
            elif k == 2 or (k == 3 and i < early):
                nc.gpsimd.tensor_scalar(
                    out=term[:],
                    in0=rows[:, k - 1, :],
                    scalar1=LARGEST,
                    scalar2=xs[:, i, d : d + 1],
                    op0=ALU.min,
                    op1=ALU.max,
                )
            else:
                nc.scalar.activation(
                    out=term[:],
                    in_=rows[:, k - 1, :],
                    func=ACT.Abs,
                    scale=0.5,
                    bias=neg_half[:, i, d : d + 1],
                )

        def start_early(i, d):
            terms[i, "early", d] = work.tile([P, M_PTS], F32, name="early%d" % d)
            nc.scalar.activation(
                out=terms[i, "early", d][:],
                in_=z_rows[d][:],
                func=ACT.Abs,
                scale=0.5,
                bias=neg_half[:, i, d : d + 1],
            )

        def is_shared(i):
            return i < N_TILES - UNSHARED

        def extend_term(i, k, d, halves=BOTH):
            start, end = halves[0] * K_PASS, (halves[-1] + 1) * K_PASS
            if d == SHARED and is_shared(i):
                start, end = max(start, VECTOR_FROM * P), min(end, VECTOR_TO * P)
            term = terms[i, k][:, start:end]
            nc.vector.scalar_tensor_tensor(
                out=term,
                in0=z_rows[d][:, start:end],
                scalar=xs[:, i, d : d + 1],
                in1=term,
                op0=ALU.max,
                op1=ALU.add,
            )

        def start_shared(i):
            terms[i, 0] = work.tile([P, len(SHORT_SLABS), P], F32, name="term0")
            nc.gpsimd.tensor_scalar(
                out=terms[i, 0][:],
                in0=shared_row[:],
                scalar1=LARGEST,
                scalar2=xs[:, i, SHARED : SHARED + 1],
                op0=ALU.min,
                op1=ALU.max,
            )

        def sum_half(i, g):
            bank = psum.tile([P, PACK, P], F32, name="half_l1", tag="sum%d" % g)
            half_l1[i, g] = bank
            if i < early:
                sources = [terms[i, 4][:]] + [terms[i, "early", d][:] for d in EARLY[i]]
                sources += [terms[i, k][:] for k in ((3, 1, 2) if i == 0 else (1, 2, 3))]
            else:
                sources = [terms[i, k][:] for k in TERM_ORDER]
            short = [j for j, slab in enumerate(SHORT_SLABS) if is_shared(i) and slab // PACK == g]
            for place, source in enumerate(sources):
                if i < early and place % 3 == 2:
                    keep_warm(idle_bank)
                for t in range(PACK):
                    slab = g * PACK + t
                    nc.tensor.matmul(
                        out=bank[:, t, :],
                        lhsT=source[:, slab * P : (slab + 1) * P],
                        rhs=identity[:],
                        is_transpose=True,
                        start=(place == 0 and t == 0),
                        stop=(place == len(sources) - 1 and t == PACK - 1 and not short),
                    )
            for j in short:
                nc.tensor.matmul(
                    out=bank[:, SHORT_SLABS[j] % PACK, :],
                    lhsT=terms[i, 0][:, j, :],
                    rhs=identity[:],
                    is_transpose=True,
                    start=False,
                    stop=(j == short[-1]),
                )

        def exponential(i, g):
            if g == 0:
                planar[i] = work.tile([P, PASSES, PACK, P], BF16, name="planar")
            for t in range(PACK):
                slab = g * PACK + t
                nc.scalar.activation(
                    out=planar[i][:, g, t, :],
                    in_=half_l1[i, g][:, t, :],
                    func=ACT.Exp,
                    scale=-2.0,
                    bias=z_sum[len(EARLY[i]) if i < early else 0][:, slab : slab + 1],
                )

        def interleave(i):
            k_star[i] = single.tile([P, PASSES, P, PACK], BF16, name="k_star", align_bytes=64)
            nc.gpsimd.tensor_scalar(
                out=k_star[i][:],
                in0=planar[i][:].rearrange("p g t n -> p g n t"),
                scalar1=1.0,
                scalar2=0.0,
                op0=ALU.mult,
                op1=ALU.add,
            )

        def interleave_last(g):
            if g == 0:
                k_star[last] = single.tile([P, PASSES, P, PACK], BF16, name="k_star_last", align_bytes=64)
            nc.vector.tensor_copy(
                out=k_star[last][:, g, :, :], in_=planar[last][:, g, :, :].rearrange("p t n -> p n t")
            )

        def quantise(i, halves=BOTH):
            if i not in k_words:
                k_words[i] = work.tile([P, PASSES * P], U32, name="k_words", align_bytes=64)
                k_scales[i] = work.tile([P, PASSES * P], U8, name="k_scales", align_bytes=64)
            some = slice(halves[0], halves[-1] + 1)
            columns = slice(halves[0] * P, (halves[-1] + 1) * P)
            nc.vector.quantize_mx(
                out=k_words[i][:, columns].bitcast(FP8X4),
                scales=k_scales[i][:, columns],
                in_=k_star[i][:, some, :, :].rearrange("p g n t -> p (g n t)"),
            )

        def open_product(i, h, tag):
            acc[i, h] = psum.tile([P, BANK], F32, name="acc", tag=tag)

        def multiply_pass(i, h, g):
            nc.tensor.matmul_mx(
                out=acc[i, h][:],
                lhsT=k_words[i][:, g * P : (g + 1) * P].bitcast(FP8X4),
                lhsT_scale=k_scales[i][:, g * P : (g + 1) * P],
                rhs=w_words[:, g, h * BANK : (h + 1) * BANK].bitcast(FP8X4),
                rhs_scale=w_scales[:, g, h * BANK : (h + 1) * BANK],
                start=(g == 0),
                stop=(g == PASSES - 1),
            )

        def multiply(i, h):
            open_product(i, h, "acc%d" % h)
            for g in range(PASSES):
                multiply_pass(i, h, g)

        def copy_out(i, h, on_vector=False):
            if h == 0:
                result[i] = work.tile([P, N_COLS], F32, name="result", bufs=4)
            columns = slice(h * BANK, (h + 1) * BANK)
            if on_vector:
                nc.vector.tensor_copy(out=result[i][:, columns], in_=acc[i, h][:])
            else:
                nc.scalar.copy(out=result[i][:, columns], in_=acc[i, h][:])

        def store(i, columns=slice(0, N_COLS)):
            nc.sync.dma_start(out=out_tiles[i][:, columns], in_=result[i][:, columns])

        def live(i):
            return 0 <= i < N_TILES

        start_term(0, 2)
        start_term(0, 3)
        start_term(0, 1)
        start_term(0, 4)
        nc.scalar.copy(out=shared_row[:, 0, :], in_=z_rows[SHARED][:, 0:P])
        nc.scalar.copy(
            out=shared_row[:, 1:3, :].rearrange("p s c -> p (s c)"),
            in_=z_rows[SHARED][:, VECTOR_TO * P : M_PTS],
        )
        start_shared(0)
        for d in EARLY[0]:
            start_early(0, d)
        nc.scalar.activation(
            out=neg_half[:, early:N_TILES, :], in_=xs[:, early:N_TILES, :], func=ACT.Copy, scale=-0.5
        )
        nc.vector.tensor_reduce(
            out=xs_sum[:, early:N_TILES], in_=xs[:, early:N_TILES, 0:MAX_DIMS], axis=AXIS_X, op=ALU.add
        )
        nc.vector.tensor_scalar_mul(
            out=shift[:, early:N_TILES], in0=xs_sum[:, early:N_TILES], scalar1=-0.5
        )
        extend_term(0, 1, 2)
        extend_term(0, 2, 3)

        last = N_TILES - 1
        for step in range(N_TILES):
            if live(step - 3):
                quantise(step - 3)
            if live(step - 2):
                interleave(step - 2)
            if live(step + 1):
                start_term(step + 1, 2)
                if step + 1 < early:
                    start_term(step + 1, 3)
                if is_shared(step + 1):
                    start_shared(step + 1)
            for half in range(2):
                if half == 0 and live(step - 4):
                    copy_out(step - 4, 1)
                    store(step - 4)
                if half == 1 and live(step - 3):
                    copy_out(step - 3, 0)
                if half == 0 and step + 1 < early:
                    start_early(step + 1, 0)
                elif live(step + 1):
                    start_term(step + 1, 3 + half)
                if live(step - 1):
                    sum_half(step - 1, half)
                if live(step - 3):
                    multiply(step - 3, half)
                if live(step - 1):
                    exponential(step - 1, half)
            if 0 < step < last:
                start_term(step, 1)
                if step < early:
                    for k in (1, 2, 3):
                        extend_term(step, k, k)
                else:
                    for k in TERM_ORDER:
                        extend_term(step, k, k - 1)
        copy_out(last - 3, 1)
        store(last - 3)
        for g in range(PASSES):
            start_term(last, 1, (g,))
            for k in TERM_ORDER:
                extend_term(last, k, k - 1, (g,))
            sum_half(last, g)
            exponential(last, g)
            if g == 0:
                quantise(last - 2)
                interleave(last - 1)
        for h in range(HALVES):
            multiply(last - 2, h)
        quantise(last - 1)
        for g in range(PASSES):
            interleave_last(g)
            quantise(last, (g,))
        for h in range(HALVES):
            copy_out(last - 2, h, on_vector=(h == 1))
        store(last - 2)
        for h in range(HALVES):
            open_product(last - 1, h, "z_row%d" % h)
            open_product(last, h, "z_row%d" % (2 + h))
        for h in range(HALVES):
            for g in range(PASSES):
                multiply_pass(last - 1, h, g)
        for h in range(HALVES):
            copy_out(last - 1, h, on_vector=(h == 1))
        store(last - 1)
        for g in range(PASSES):
            for h in range(HALVES):
                multiply_pass(last, h, g)
        for h in range(HALVES):
            copy_out(last, h, on_vector=(h == 1))
            store(last, slice(h * BANK, (h + 1) * BANK))
